import numpy as np
import ml_dtypes


def mxq(x, axis, fmt="e4m3"):
    dtype, down = {"e4m3": (ml_dtypes.float8_e4m3fn, 7), "e5m2": (ml_dtypes.float8_e5m2, 14)}[fmt]
    v = np.moveaxis(np.asarray(x, np.float32).astype(ml_dtypes.bfloat16).astype(np.float64), axis, -1)
    blocks = v.reshape(v.shape[:-1] + (-1, 32))
    amax = np.abs(blocks).max(-1, keepdims=True)
    byte = np.maximum(np.where(amax > 0, np.frexp(amax)[1] - 1 + 127, 0) - down, 1)
    scale = np.exp2(byte - 127.0)
    codes = (blocks / scale).astype(np.float32).astype(dtype).astype(np.float64)
    return np.moveaxis((codes * scale).reshape(v.shape), -1, axis)


WIDE = False


def mx_kscale(k):
    if not WIDE:
        return np.ones(k)
    levels = np.array([10, -10, 5, -5, 0])
    if k % 512:
        return np.exp2(np.random.permutation(np.resize(levels, k // 32))).repeat(32)
    a = np.empty((k // 512, 16))
    for p in range(k // 512):
        a[p, :8] = np.random.permutation(np.resize(levels, 8))
        for g in range(8):
            far = levels[np.abs(levels - a[p, g]) >= 10]
            a[p, g + 8] = far[np.random.randint(len(far))]
    return np.exp2(a.ravel()).repeat(32)


BF16 = ml_dtypes.bfloat16


def bf(x):
    return np.asarray(x, np.float32).astype(BF16)


def f64(x):
    return np.asarray(x).astype(np.float64)


B, T, KA, KT, DIM, NH, HD, E = 2, 256, 128, 128, 512, 8, 64, 8
EPS = 1e-5


def setup_inputs():
    r = np.random.standard_normal
    s = mx_kscale(DIM)
    t = mx_kscale(DIM)
    return {"h_attn": bf(r((B, T, DIM)) * 0.4 * s),
            "x": bf(r((B, T, DIM))),
            "W_o": bf(r((DIM, DIM)) * 2.0 / np.sqrt(DIM) / s[None, :]),
            "b_o": bf(r(DIM) * 0.3 + 0.2),
            "W_ffn": bf(r((DIM, DIM)) / np.sqrt(DIM) / t[None, :]),
            "b_ffn": bf(r(DIM) * 0.3),
            "gamma": bf((1.0 + 0.1 * r(DIM)) * t),
            "beta": bf(0.2 * r(DIM) * t)}


def reference(h_attn, x, W_o, b_o, W_ffn, b_ffn, gamma, beta):
    y = (mxq(f64(h_attn), 2, "e4m3") @ mxq(f64(W_o), 1, "e4m3").T) + f64(b_o) + f64(x)
    mu = y.mean(-1, keepdims=True)
    var = ((y - mu) ** 2).mean(-1, keepdims=True)
    xn = (y - mu) / np.sqrt(var + EPS) * f64(gamma) + f64(beta)
    return np.maximum((mxq(xn, 2, "e4m3") @ mxq(f64(W_ffn), 1, "e4m3").T) + f64(b_ffn), 0.0)

@@ -1,0 +1,215 @@
+from contextlib import ExitStack
+
+import concourse.mybir as mybir
+from concourse.masks import make_identity
+
+F32 = mybir.dt.float32
+BF16 = mybir.dt.bfloat16
+U32 = mybir.dt.uint32
+U8 = mybir.dt.uint8
+FP8X4 = mybir.dt.float8_e4m3fn_x4
+ALU = mybir.AluOpType
+ACT = mybir.ActivationFunctionType
+
+P = 128
+DIM = 512
+ROWS = 512
+ROW_TILES = ROWS // P
+PACK = 4
+WORD_RUNS = 2
+HALF_TILES = 2
+HALF_ROWS = HALF_TILES * P
+EPS = 1e-5
+
+FLOPS = 2 * 2 * ROWS * DIM * DIM
+
+
+def tile_l1regressionmoeactionhead_pc_s_kernel(
+    tc, h_attn, x, W_o, b_o, W_ffn, b_ffn, gamma, beta, out
+):
+    nc = tc.nc
+    with ExitStack() as ctx:
+        keep = ctx.enter_context(tc.tile_pool(name="keep", bufs=1))
+        psum = ctx.enter_context(tc.psum_pool(name="psum", bufs=8))
+        ctx.enter_context(tc.manual_schedule())
+
+        h_view = h_attn.flatten_outer_dims().rearrange("(p j) k -> p j k", j=ROW_TILES)
+        x_view = x.flatten_outer_dims().rearrange("(p j) o -> p j o", j=ROW_TILES)
+        out_view = out.flatten_outer_dims().rearrange("(p j) f -> p j f", j=ROW_TILES)
+        wo_view = W_o.rearrange("(j p) k -> p j k", p=P)
+        wf_view = W_ffn.rearrange("(j p) k -> p j k", p=P)
+
+        def load_half(sb, view, half):
+            tiles = slice(half * HALF_TILES, (half + 1) * HALF_TILES)
+            nc.sync.dma_start(out=sb[:, tiles, :], in_=view[:, tiles, :])
+
+        vec_rows = keep.tile([P, DIM // WORD_RUNS], BF16)
+        nc.gpsimd.memset(vec_rows[:], 0.0)
+        for v, vec in enumerate((b_o, gamma, beta, b_ffn)):
+            nc.sync.dma_start(
+                out=vec_rows[WORD_RUNS * v : WORD_RUNS * (v + 1), :],
+                in_=vec.rearrange("(u c) -> u c", u=WORD_RUNS),
+            )
+        wo_sb = keep.tile([P, ROW_TILES, DIM], BF16)
+        h_sb = keep.tile([P, ROW_TILES, DIM], BF16)
+        x_sb = keep.tile([P, ROW_TILES, DIM], BF16)
+        wf_sb = keep.tile([P, ROW_TILES, DIM], BF16)
+        nc.sync.dma_start(out=x_sb[:], in_=x_view)
+        load_half(wo_sb, wo_view, 0)
+        load_half(wo_sb, wo_view, 1)
+        load_half(h_sb, h_view, 0)
+        load_half(h_sb, h_view, 1)
+        load_half(wf_sb, wf_view, 0)
+        load_half(wf_sb, wf_view, 1)
+
+        ident_f32 = keep.tile([P, P], F32)
+        make_identity(nc, ident_f32[:])
+        eps = keep.tile([P, 1], F32)
+        nc.vector.memset(eps[:], EPS)
+        warm = keep.tile([P, 1], F32)
+        nc.scalar.activation(out=warm[:], in_=eps[:], func=ACT.Sqrt)
+
+        def mx_tiles(name):
+            grouped = keep.tile([P, ROWS, PACK], BF16, align_bytes=64, name=name + "_grouped")
+            codes = keep.tile([P, ROWS], U32, align_bytes=64, name=name + "_codes")
+            scales = keep.tile([P, ROWS], U8, align_bytes=64, name=name + "_scales")
+            return grouped, codes, scales
+
+        def regroup(operand, first_col, row_tiles):
+            n = len(row_tiles)
+            bank = psum.tile([P, n, WORD_RUNS, P], F32, tag="bank")
+            for i, rows in enumerate(row_tiles):
+                words = rows.bitcast(F32)
+                for u in range(WORD_RUNS):
+                    nc.tensor.transpose(bank[:, i, u, :], words[:, u : WORD_RUNS * P : WORD_RUNS], ident_f32[:])
+            nc.scalar.copy(
+                out=operand[0][:].bitcast(F32)[:, first_col : first_col + n * P, :].rearrange(
+                    "p (i r) u -> p i r u", i=n
+                ),
+                in_=bank[:].rearrange("p i u r -> p i r u"),
+            )
+
+        def regroup_half(operand, sb, half):
+            first = half * HALF_TILES
+            regroup(operand, first * P, [sb[:, first + i, :] for i in range(HALF_TILES)])
+
+        def quantise(operand, first_col, n_cols):
+            grouped, codes, scales = operand
+            cols = slice(first_col, first_col + n_cols)
+            nc.vector.quantize_mx(
+                out=codes[:, cols].bitcast(FP8X4),
+                scales=scales[:, cols],
+                in_=grouped[:, cols, :].rearrange("p r t -> p (r t)"),
+            )
+
+        def multiply(tokens_operand, j, weights_operand):
+            toks = slice(j * P, (j + 1) * P)
+            acc = psum.tile([P, DIM], F32, tag="bank")
+            nc.tensor.matmul_mx(
+                out=acc[:],
+                lhsT=tokens_operand[1][:, toks].bitcast(FP8X4),
+                lhsT_scale=tokens_operand[2][:, toks],
+                rhs=weights_operand[1][:].bitcast(FP8X4),
+                rhs_scale=weights_operand[2][:],
+                start=True,
+                stop=True,
+            )
+            return acc
+
+        vec_bank = psum.tile([P, P], F32, tag="bank")
+        nc.tensor.transpose(vec_bank[:], vec_rows[:].bitcast(F32), ident_f32[:])
+        vec_cols = keep.tile([P, 4 * WORD_RUNS], F32)
+        nc.vector.tensor_copy(out=vec_cols[:], in_=vec_bank[:, 0 : 4 * WORD_RUNS])
+        spread_all = keep.tile([P, 4, DIM], BF16)
+
+        def spread(first, n):
+            bank = psum.tile([P, n * WORD_RUNS, P], F32, tag="bank")
+            for i in range(n * WORD_RUNS):
+                col = first * WORD_RUNS + i
+                nc.tensor.transpose(
+                    bank[:, i, :], vec_cols[:, col : col + 1].to_broadcast([P, P]), ident_f32[:]
+                )
+            nc.scalar.copy(
+                out=spread_all[:, first : first + n, :].bitcast(F32).rearrange("p v w -> p (v w)"),
+                in_=bank[:].rearrange("p i c -> p (i c)"),
+            )
+
+        gamma_all = spread_all[:, 1, :]
+        beta_all = spread_all[:, 2, :]
+        b_ffn_all = spread_all[:, 3, :]
+
+        wo_mx = mx_tiles("wo")
+        h_mx = mx_tiles("h")
+        wf_mx = mx_tiles("wf")
+        xn_mx = mx_tiles("xn")
+
+        xb = keep.tile([P, ROW_TILES, DIM], F32)
+        y = keep.tile([P, ROW_TILES, DIM], F32)
+        y_sum = keep.tile([P, ROW_TILES], F32)
+        squares = keep.tile([P, ROW_TILES, DIM], BF16)
+        sq_sum = keep.tile([P, ROW_TILES], F32)
+
+        def residual_and_sums(j):
+            y_acc = multiply(h_mx, j, wo_mx)
+            nc.vector.scalar_tensor_tensor(
+                out=y[:, j, :], in0=y_acc[:], scalar=0.0, in1=xb[:, j, :],
+                op0=ALU.add, op1=ALU.add, accum_out=y_sum[:, j : j + 1],
+            )
+            nc.scalar.activation(
+                out=squares[:, j, :], in_=y[:, j, :], func=ACT.Square,
+                bias=y_sum[:, j : j + 1], scale=-1.0 * DIM, accum_out=sq_sum[:, j : j + 1],
+            )
+
+        spread(0, 1)
+        nc.vector.tensor_tensor(
+            out=xb[:], in0=x_sb[:], in1=spread_all[:, 0:1, :].to_broadcast([P, ROW_TILES, DIM]), op=ALU.add
+        )
+        spread(1, 2)
+        for half in range(2):
+            regroup_half(wo_mx, wo_sb, half)
+        for half in range(2):
+            quantise(wo_mx, half * HALF_ROWS, HALF_ROWS)
+        for j in range(ROW_TILES):
+            regroup(h_mx, j * P, [h_sb[:, j, :]])
+            quantise(h_mx, j * P, P)
+        for j in range(ROW_TILES):
+            residual_and_sums(j)
+
+        neg_mean = keep.tile([P, ROW_TILES], F32)
+        nc.vector.tensor_scalar_mul(out=neg_mean[:], in0=y_sum[:], scalar1=-1.0 / DIM)
+        std = keep.tile([P, ROW_TILES], F32)
+        nc.scalar.activation(
+            out=std[:], in_=sq_sum[:], func=ACT.Sqrt, bias=eps[:], scale=1.0 / (DIM * DIM * DIM)
+        )
+        rstd = keep.tile([P, ROW_TILES], F32)
+
+        for half in range(2):
+            regroup_half(wf_mx, wf_sb, half)
+        spread(3, 1)
+
+        gained = keep.tile([P, ROW_TILES, DIM], F32)
+        for j in range(ROW_TILES):
+            nc.vector.scalar_tensor_tensor(
+                out=gained[:, j, :], in0=y[:, j, :], scalar=neg_mean[:, j : j + 1], in1=gamma_all,
+                op0=ALU.add, op1=ALU.mult,
+            )
+        nc.vector.reciprocal(rstd[:], std[:])
+        xn = keep.tile([P, ROW_TILES, DIM], BF16)
+        for j in range(ROW_TILES):
+            nc.vector.scalar_tensor_tensor(
+                out=xn[:, j, :], in0=gained[:, j, :], scalar=rstd[:, j : j + 1], in1=beta_all,
+                op0=ALU.mult, op1=ALU.add,
+            )
+            regroup(xn_mx, j * P, [xn[:, j, :]])
+
+        quantise(wf_mx, 0, ROWS)
+        biased = keep.tile([P, ROW_TILES, DIM], F32)
+        result = keep.tile([P, ROW_TILES, DIM], F32)
+        o_accs = []
+        for j in range(ROW_TILES):
+            quantise(xn_mx, j * P, P)
+            o_accs.append(multiply(xn_mx, j, wf_mx))
+        for j in range(ROW_TILES):
+            nc.vector.tensor_tensor(out=biased[:, j, :], in0=o_accs[j][:], in1=b_ffn_all, op=ALU.add)
+            nc.scalar.activation(out=result[:, j, :], in_=biased[:, j, :], func=ACT.Relu)
+            nc.sync.dma_start(out=out_view[:, j, :], in_=result[:, j, :])

@@ -16,9 +16,7 @@ DIM = 512
 ROWS = 512
 ROW_TILES = ROWS // P
 PACK = 4
-WORD_RUNS = 2
 HALF_TILES = 2
-HALF_ROWS = HALF_TILES * P
 EPS = 1e-5
 
 FLOPS = 2 * 2 * ROWS * DIM * DIM
@@ -43,31 +41,39 @@ def tile_l1regressionmoeactionhead_pc_s_kernel(
             tiles = slice(half * HALF_TILES, (half + 1) * HALF_TILES)
             nc.sync.dma_start(out=sb[:, tiles, :], in_=view[:, tiles, :])
 
-        vec_rows = keep.tile([P, DIM // WORD_RUNS], BF16)
-        nc.gpsimd.memset(vec_rows[:], 0.0)
-        for v, vec in enumerate((b_o, gamma, beta, b_ffn)):
-            nc.sync.dma_start(
-                out=vec_rows[WORD_RUNS * v : WORD_RUNS * (v + 1), :],
-                in_=vec.rearrange("(u c) -> u c", u=WORD_RUNS),
-            )
+        def load_vec(vec, name):
+            rows = keep.tile([P, DIM], BF16, name=name)
+            nc.gpsimd.memset(rows[:].bitcast(F32), 0.0)
+            nc.sync.dma_start(out=rows[0:1, :], in_=vec.rearrange("(u c) -> u c", u=1))
+            return rows
+
         wo_sb = keep.tile([P, ROW_TILES, DIM], BF16)
         h_sb = keep.tile([P, ROW_TILES, DIM], BF16)
         x_sb = keep.tile([P, ROW_TILES, DIM], BF16)
         wf_sb = keep.tile([P, ROW_TILES, DIM], BF16)
-        nc.sync.dma_start(out=x_sb[:], in_=x_view)
+        b_ffn_all = keep.tile([P, DIM], BF16)
+        b_o_cols = keep.tile([P, PACK], BF16)
+        nc.sync.dma_start(out=b_o_cols[:], in_=b_o.rearrange("(q t) -> q t", t=PACK))
+        load_half(x_sb, x_view, 0)
         load_half(wo_sb, wo_view, 0)
+        load_half(x_sb, x_view, 1)
         load_half(wo_sb, wo_view, 1)
         load_half(h_sb, h_view, 0)
         load_half(h_sb, h_view, 1)
+        gamma_rows = load_vec(gamma, "gamma_rows")
+        beta_rows = load_vec(beta, "beta_rows")
         load_half(wf_sb, wf_view, 0)
         load_half(wf_sb, wf_view, 1)
+        nc.sync.dma_start(out=b_ffn_all[:], in_=b_ffn.partition_broadcast(P))
 
         ident_f32 = keep.tile([P, P], F32)
         make_identity(nc, ident_f32[:])
         eps = keep.tile([P, 1], F32)
         nc.vector.memset(eps[:], EPS)
+        ones = keep.tile([P, P], BF16)
+        nc.vector.memset(ones[:], 1.0)
         warm = keep.tile([P, 1], F32)
-        nc.scalar.activation(out=warm[:], in_=eps[:], func=ACT.Sqrt)
+        nc.scalar.activation(out=warm[:], in_=eps[:], func=ACT.Abs_reciprocal_sqrt)
 
         def mx_tiles(name):
             grouped = keep.tile([P, ROWS, PACK], BF16, align_bytes=64, name=name + "_grouped")
@@ -75,23 +81,22 @@ def tile_l1regressionmoeactionhead_pc_s_kernel(
             scales = keep.tile([P, ROWS], U8, align_bytes=64, name=name + "_scales")
             return grouped, codes, scales
 
-        def regroup(operand, first_col, row_tiles):
+        def turn(row_tiles):
             n = len(row_tiles)
-            bank = psum.tile([P, n, WORD_RUNS, P], F32, tag="bank")
+            bank = psum.tile([P, n, 2, P], F32, tag="bank")
             for i, rows in enumerate(row_tiles):
                 words = rows.bitcast(F32)
-                for u in range(WORD_RUNS):
-                    nc.tensor.transpose(bank[:, i, u, :], words[:, u : WORD_RUNS * P : WORD_RUNS], ident_f32[:])
+                for u in range(2):
+                    nc.tensor.transpose(bank[:, i, u, :], words[:, u : 2 * P : 2], ident_f32[:])
+            return bank
+
+        def group(operand, first_col, bank, n):
             nc.scalar.copy(
                 out=operand[0][:].bitcast(F32)[:, first_col : first_col + n * P, :].rearrange(
                     "p (i r) u -> p i r u", i=n
                 ),
                 in_=bank[:].rearrange("p i u r -> p i r u"),
             )
-
-        def regroup_half(operand, sb, half):
-            first = half * HALF_TILES
-            regroup(operand, first * P, [sb[:, first + i, :] for i in range(HALF_TILES)])
 
         def quantise(operand, first_col, n_cols):
             grouped, codes, scales = operand
@@ -116,27 +121,10 @@ def tile_l1regressionmoeactionhead_pc_s_kernel(
             )
             return acc
 
-        vec_bank = psum.tile([P, P], F32, tag="bank")
-        nc.tensor.transpose(vec_bank[:], vec_rows[:].bitcast(F32), ident_f32[:])
-        vec_cols = keep.tile([P, 4 * WORD_RUNS], F32)
-        nc.vector.tensor_copy(out=vec_cols[:], in_=vec_bank[:, 0 : 4 * WORD_RUNS])
-        spread_all = keep.tile([P, 4, DIM], BF16)
-
-        def spread(first, n):
-            bank = psum.tile([P, n * WORD_RUNS, P], F32, tag="bank")
-            for i in range(n * WORD_RUNS):
-                col = first * WORD_RUNS + i
-                nc.tensor.transpose(
-                    bank[:, i, :], vec_cols[:, col : col + 1].to_broadcast([P, P]), ident_f32[:]
-                )
-            nc.scalar.copy(
-                out=spread_all[:, first : first + n, :].bitcast(F32).rearrange("p v w -> p (v w)"),
-                in_=bank[:].rearrange("p i c -> p (i c)"),
-            )
-
-        gamma_all = spread_all[:, 1, :]
-        beta_all = spread_all[:, 2, :]
-        b_ffn_all = spread_all[:, 3, :]
+        def spread(rows):
+            bank = psum.tile([P, 1, DIM], F32, tag="bank")
+            nc.tensor.matmul(bank[:, 0, :], lhsT=ones[:], rhs=rows[:], start=True, stop=True)
+            return bank
 
         wo_mx = mx_tiles("wo")
         h_mx = mx_tiles("h")
@@ -148,11 +136,49 @@ def tile_l1regressionmoeactionhead_pc_s_kernel(
         y_sum = keep.tile([P, ROW_TILES], F32)
         squares = keep.tile([P, ROW_TILES, DIM], BF16)
         sq_sum = keep.tile([P, ROW_TILES], F32)
+        neg_mean = keep.tile([P, ROW_TILES], F32)
+        rstd = keep.tile([P, ROW_TILES], F32)
+        gained = keep.tile([P, ROW_TILES, DIM], F32)
+        xn = keep.tile([P, ROW_TILES, DIM], BF16)
+        biased = keep.tile([P, ROW_TILES, DIM], F32)
+        result = keep.tile([P, ROW_TILES, DIM], F32)
 
-        def residual_and_sums(j):
-            y_acc = multiply(h_mx, j, wo_mx)
+        b_o_bank = psum.tile([P, 2, P], F32, tag="bank")
+        for u in range(2):
+            nc.tensor.transpose(
+                b_o_bank[:, u, :], b_o_cols[:].bitcast(F32)[:, u : u + 1].to_broadcast([P, P]), ident_f32[:]
+            )
+        b_o_all = b_o_bank[:].bitcast(BF16).rearrange("p u (q e) -> p q u e", e=2)
+
+        def add_b_o(j):
+            split = "p (q u e) -> p q u e"
+            nc.vector.tensor_tensor(
+                out=xb[:, j, :].rearrange(split, u=2, e=2), in0=x_sb[:, j, :].rearrange(split, u=2, e=2),
+                in1=b_o_all, op=ALU.add,
+            )
+
+        for j in range(ROW_TILES):
+            add_b_o(j)
+        for half in range(2):
+            first = half * HALF_TILES
+            bank = turn([wo_sb[:, first + i, :] for i in range(HALF_TILES)])
+            group(wo_mx, first * P, bank, HALF_TILES)
+        for half in range(2):
+            quantise(wo_mx, half * HALF_TILES * P, HALF_TILES * P)
+        for j in range(ROW_TILES):
+            bank = turn([h_sb[:, j, :]])
+            group(h_mx, j * P, bank, 1)
+        quantise(h_mx, 0, P)
+        quantise(h_mx, P, P)
+        quantise(h_mx, 2 * P, P)
+        quantise(h_mx, 3 * P, P)
+        accs = [multiply(h_mx, j, wo_mx) for j in range(ROW_TILES)]
+        gamma_bank = spread(gamma_rows)
+        beta_bank = spread(beta_rows)
+
+        def residual(j):
             nc.vector.scalar_tensor_tensor(
-                out=y[:, j, :], in0=y_acc[:], scalar=0.0, in1=xb[:, j, :],
+                out=y[:, j, :], in0=accs[j][:], scalar=0.0, in1=xb[:, j, :],
                 op0=ALU.add, op1=ALU.add, accum_out=y_sum[:, j : j + 1],
             )
             nc.scalar.activation(
@@ -160,56 +186,74 @@ def tile_l1regressionmoeactionhead_pc_s_kernel(
                 bias=y_sum[:, j : j + 1], scale=-1.0 * DIM, accum_out=sq_sum[:, j : j + 1],
             )
 
-        spread(0, 1)
-        nc.vector.tensor_tensor(
-            out=xb[:], in0=x_sb[:], in1=spread_all[:, 0:1, :].to_broadcast([P, ROW_TILES, DIM]), op=ALU.add
-        )
-        spread(1, 2)
-        for half in range(2):
-            regroup_half(wo_mx, wo_sb, half)
-        for half in range(2):
-            quantise(wo_mx, half * HALF_ROWS, HALF_ROWS)
-        for j in range(ROW_TILES):
-            regroup(h_mx, j * P, [h_sb[:, j, :]])
-            quantise(h_mx, j * P, P)
-        for j in range(ROW_TILES):
-            residual_and_sums(j)
+        def negate_mean(first, n):
+            cols = slice(first, first + n)
+            nc.vector.tensor_scalar_mul(out=neg_mean[:, cols], in0=y_sum[:, cols], scalar1=-1.0 / DIM)
 
-        neg_mean = keep.tile([P, ROW_TILES], F32)
-        nc.vector.tensor_scalar_mul(out=neg_mean[:], in0=y_sum[:], scalar1=-1.0 / DIM)
-        std = keep.tile([P, ROW_TILES], F32)
-        nc.scalar.activation(
-            out=std[:], in_=sq_sum[:], func=ACT.Sqrt, bias=eps[:], scale=1.0 / (DIM * DIM * DIM)
-        )
-        rstd = keep.tile([P, ROW_TILES], F32)
+        def spread_rstd(first, n):
+            cols = slice(first, first + n)
+            nc.scalar.activation(
+                out=rstd[:, cols], in_=sq_sum[:, cols], func=ACT.Abs_reciprocal_sqrt,
+                bias=eps[:], scale=1.0 / (DIM * DIM * DIM),
+            )
 
-        for half in range(2):
-            regroup_half(wf_mx, wf_sb, half)
-        spread(3, 1)
-
-        gained = keep.tile([P, ROW_TILES, DIM], F32)
-        for j in range(ROW_TILES):
+        def gain(j):
             nc.vector.scalar_tensor_tensor(
-                out=gained[:, j, :], in0=y[:, j, :], scalar=neg_mean[:, j : j + 1], in1=gamma_all,
+                out=gained[:, j, :], in0=y[:, j, :], scalar=neg_mean[:, j : j + 1], in1=gamma_bank[:, 0, :],
                 op0=ALU.add, op1=ALU.mult,
             )
-        nc.vector.reciprocal(rstd[:], std[:])
-        xn = keep.tile([P, ROW_TILES, DIM], BF16)
-        for j in range(ROW_TILES):
-            nc.vector.scalar_tensor_tensor(
-                out=xn[:, j, :], in0=gained[:, j, :], scalar=rstd[:, j : j + 1], in1=beta_all,
-                op0=ALU.mult, op1=ALU.add,
-            )
-            regroup(xn_mx, j * P, [xn[:, j, :]])
 
-        quantise(wf_mx, 0, ROWS)
-        biased = keep.tile([P, ROW_TILES, DIM], F32)
-        result = keep.tile([P, ROW_TILES, DIM], F32)
-        o_accs = []
-        for j in range(ROW_TILES):
-            quantise(xn_mx, j * P, P)
-            o_accs.append(multiply(xn_mx, j, wf_mx))
-        for j in range(ROW_TILES):
-            nc.vector.tensor_tensor(out=biased[:, j, :], in0=o_accs[j][:], in1=b_ffn_all, op=ALU.add)
+        def normalise(j):
+            nc.vector.scalar_tensor_tensor(
+                out=xn[:, j, :], in0=gained[:, j, :], scalar=rstd[:, j : j + 1],
+                in1=beta_bank[:, 0, :], op0=ALU.mult, op1=ALU.add,
+            )
+
+        residual(0)
+        residual(1)
+        spread_rstd(0, 2)
+        residual(2)
+        negate_mean(0, 2)
+        residual(3)
+        spread_rstd(2, 2)
+        gain(0)
+        negate_mean(2, 2)
+        gain(1)
+        for half in range(2):
+            first = half * HALF_TILES
+            bank = turn([wf_sb[:, first + i, :] for i in range(HALF_TILES)])
+            group(wf_mx, first * P, bank, HALF_TILES)
+        gain(2)
+        gain(3)
+
+        def turn_xn(j):
+            bank = turn([xn[:, j, :]])
+            group(xn_mx, j * P, bank, 1)
+
+        def finish(j):
+            nc.vector.tensor_tensor(out=biased[:, j, :], in0=o_accs[j][:], in1=b_ffn_all[:], op=ALU.add)
             nc.scalar.activation(out=result[:, j, :], in_=biased[:, j, :], func=ACT.Relu)
             nc.sync.dma_start(out=out_view[:, j, :], in_=result[:, j, :])
+
+        o_accs = []
+        normalise(0)
+        turn_xn(0)
+        normalise(1)
+        turn_xn(1)
+        quantise(wf_mx, 0, ROWS)
+        quantise(xn_mx, 0, P)
+        o_accs.append(multiply(xn_mx, 0, wf_mx))
+        normalise(2)
+        turn_xn(2)
+        quantise(xn_mx, P, P)
+        o_accs.append(multiply(xn_mx, 1, wf_mx))
+        normalise(3)
+        turn_xn(3)
+        finish(0)
+        quantise(xn_mx, 2 * P, P)
+        o_accs.append(multiply(xn_mx, 2, wf_mx))
+        finish(1)
+        quantise(xn_mx, 3 * P, P)
+        o_accs.append(multiply(xn_mx, 3, wf_mx))
+        finish(2)
+        finish(3)

@@ -18,6 +18,7 @@ ROW_TILES = ROWS // P
 PACK = 4
 HALF_TILES = 2
 EPS = 1e-5
+IDLE_TURNS = 6
 
 FLOPS = 2 * 2 * ROWS * DIM * DIM
 
@@ -42,36 +43,33 @@ def tile_l1regressionmoeactionhead_pc_s_kernel(
             nc.sync.dma_start(out=sb[:, tiles, :], in_=view[:, tiles, :])
 
         def load_vec(vec, name):
-            rows = keep.tile([P, DIM], BF16, name=name)
-            nc.gpsimd.memset(rows[:].bitcast(F32), 0.0)
-            nc.sync.dma_start(out=rows[0:1, :], in_=vec.rearrange("(u c) -> u c", u=1))
-            return rows
+            cols = keep.tile([P, PACK], BF16, name=name)
+            nc.sync.dma_start(out=cols[:], in_=vec.rearrange("(q t) -> q t", t=PACK))
+            return cols
 
         wo_sb = keep.tile([P, ROW_TILES, DIM], BF16)
         h_sb = keep.tile([P, ROW_TILES, DIM], BF16)
         x_sb = keep.tile([P, ROW_TILES, DIM], BF16)
         wf_sb = keep.tile([P, ROW_TILES, DIM], BF16)
-        b_ffn_all = keep.tile([P, DIM], BF16)
-        b_o_cols = keep.tile([P, PACK], BF16)
-        nc.sync.dma_start(out=b_o_cols[:], in_=b_o.rearrange("(q t) -> q t", t=PACK))
+        b_o_cols = load_vec(b_o, "b_o_cols")
+        gamma_cols = load_vec(gamma, "gamma_cols")
+        beta_cols = load_vec(beta, "beta_cols")
         load_half(x_sb, x_view, 0)
         load_half(wo_sb, wo_view, 0)
         load_half(x_sb, x_view, 1)
         load_half(wo_sb, wo_view, 1)
         load_half(h_sb, h_view, 0)
         load_half(h_sb, h_view, 1)
-        gamma_rows = load_vec(gamma, "gamma_rows")
-        beta_rows = load_vec(beta, "beta_rows")
+        b_ffn_cols = load_vec(b_ffn, "b_ffn_cols")
         load_half(wf_sb, wf_view, 0)
         load_half(wf_sb, wf_view, 1)
-        nc.sync.dma_start(out=b_ffn_all[:], in_=b_ffn.partition_broadcast(P))
 
         ident_f32 = keep.tile([P, P], F32)
         make_identity(nc, ident_f32[:])
+        ident_bf16 = keep.tile([P, P], BF16)
+        nc.vector.tensor_copy(out=ident_bf16[:], in_=ident_f32[:])
         eps = keep.tile([P, 1], F32)
         nc.vector.memset(eps[:], EPS)
-        ones = keep.tile([P, P], BF16)
-        nc.vector.memset(ones[:], 1.0)
         warm = keep.tile([P, 1], F32)
         nc.scalar.activation(out=warm[:], in_=eps[:], func=ACT.Abs_reciprocal_sqrt)
 
@@ -121,10 +119,27 @@ def tile_l1regressionmoeactionhead_pc_s_kernel(
             )
             return acc
 
-        def spread(rows):
-            bank = psum.tile([P, 1, DIM], F32, tag="bank")
-            nc.tensor.matmul(bank[:, 0, :], lhsT=ones[:], rhs=rows[:], start=True, stop=True)
+        def spread(vecs):
+            bank = psum.tile([P, len(vecs), PACK, P], BF16, tag="bank")
+            for v, cols in enumerate(vecs):
+                for t in range(PACK):
+                    nc.tensor.transpose(
+                        bank[:, v, t, :], cols[:, t : t + 1].to_broadcast([P, P]), ident_bf16[:]
+                    )
             return bank
+
+        def in_order(bank, v):
+            return bank[:, v].rearrange("p t q -> p q t")
+
+        def by_fours(ap):
+            return ap.rearrange("p (q t) -> p q t", t=PACK)
+
+        def to_sbuf(bank, n, name):
+            rows = keep.tile([P, n, DIM], BF16, name=name)
+            nc.scalar.copy(
+                out=rows[:].rearrange("p v (q t) -> p v q t", t=PACK), in_=bank[:].rearrange("p v t q -> p v q t")
+            )
+            return rows
 
         wo_mx = mx_tiles("wo")
         h_mx = mx_tiles("h")
@@ -143,22 +158,13 @@ def tile_l1regressionmoeactionhead_pc_s_kernel(
         biased = keep.tile([P, ROW_TILES, DIM], F32)
         result = keep.tile([P, ROW_TILES, DIM], F32)
 
-        b_o_bank = psum.tile([P, 2, P], F32, tag="bank")
-        for u in range(2):
-            nc.tensor.transpose(
-                b_o_bank[:, u, :], b_o_cols[:].bitcast(F32)[:, u : u + 1].to_broadcast([P, P]), ident_f32[:]
-            )
-        b_o_all = b_o_bank[:].bitcast(BF16).rearrange("p u (q e) -> p q u e", e=2)
-
-        def add_b_o(j):
-            split = "p (q u e) -> p q u e"
-            nc.vector.tensor_tensor(
-                out=xb[:, j, :].rearrange(split, u=2, e=2), in0=x_sb[:, j, :].rearrange(split, u=2, e=2),
-                in1=b_o_all, op=ALU.add,
-            )
-
+        b_o_bank = spread([b_o_cols])
+        gain_bank = spread([gamma_cols, beta_cols])
         for j in range(ROW_TILES):
-            add_b_o(j)
+            nc.vector.tensor_tensor(
+                out=by_fours(xb[:, j, :]), in0=by_fours(x_sb[:, j, :]), in1=in_order(b_o_bank, 0),
+                op=ALU.add,
+            )
         for half in range(2):
             first = half * HALF_TILES
             bank = turn([wo_sb[:, first + i, :] for i in range(HALF_TILES)])
@@ -168,13 +174,11 @@ def tile_l1regressionmoeactionhead_pc_s_kernel(
         for j in range(ROW_TILES):
             bank = turn([h_sb[:, j, :]])
             group(h_mx, j * P, bank, 1)
-        quantise(h_mx, 0, P)
-        quantise(h_mx, P, P)
-        quantise(h_mx, 2 * P, P)
-        quantise(h_mx, 3 * P, P)
+        for j in range(ROW_TILES):
+            quantise(h_mx, j * P, P)
         accs = [multiply(h_mx, j, wo_mx) for j in range(ROW_TILES)]
-        gamma_bank = spread(gamma_rows)
-        beta_bank = spread(beta_rows)
+        gain_rows = to_sbuf(gain_bank, 2, "gain_rows")
+        b_ffn_bank = spread([b_ffn_cols])
 
         def residual(j):
             nc.vector.scalar_tensor_tensor(
@@ -199,14 +203,14 @@ def tile_l1regressionmoeactionhead_pc_s_kernel(
 
         def gain(j):
             nc.vector.scalar_tensor_tensor(
-                out=gained[:, j, :], in0=y[:, j, :], scalar=neg_mean[:, j : j + 1], in1=gamma_bank[:, 0, :],
-                op0=ALU.add, op1=ALU.mult,
+                out=by_fours(gained[:, j, :]), in0=by_fours(y[:, j, :]),
+                scalar=neg_mean[:, j : j + 1], in1=in_order(gain_bank, 0), op0=ALU.add, op1=ALU.mult,
             )
 
         def normalise(j):
             nc.vector.scalar_tensor_tensor(
-                out=xn[:, j, :], in0=gained[:, j, :], scalar=rstd[:, j : j + 1],
-                in1=beta_bank[:, 0, :], op0=ALU.mult, op1=ALU.add,
+                out=by_fours(xn[:, j, :]), in0=by_fours(gained[:, j, :]),
+                scalar=rstd[:, j : j + 1], in1=in_order(gain_bank, 1), op0=ALU.mult, op1=ALU.add,
             )
 
         residual(0)
@@ -216,44 +220,60 @@ def tile_l1regressionmoeactionhead_pc_s_kernel(
         negate_mean(0, 2)
         residual(3)
         spread_rstd(2, 2)
-        gain(0)
-        negate_mean(2, 2)
         gain(1)
+        negate_mean(2, 2)
+
+        centred = keep.tile([P, DIM], F32)
+        scaled = keep.tile([P, DIM], F32)
+        nc.gpsimd.tensor_scalar(
+            out=centred[:], in0=y[:, 0, :], scalar1=neg_mean[:, 0:1], scalar2=rstd[:, 0:1],
+            op0=ALU.add, op1=ALU.mult,
+        )
+        nc.gpsimd.tensor_tensor(out=scaled[:], in0=centred[:], in1=gain_rows[:, 0, :], op=ALU.mult)
+        nc.gpsimd.tensor_tensor(out=xn[:, 0, :], in0=scaled[:], in1=gain_rows[:, 1, :], op=ALU.add)
+
+        gain(2)
         for half in range(2):
             first = half * HALF_TILES
             bank = turn([wf_sb[:, first + i, :] for i in range(HALF_TILES)])
             group(wf_mx, first * P, bank, HALF_TILES)
-        gain(2)
+        b_ffn_rows = to_sbuf(b_ffn_bank, 1, "b_ffn_rows")
         gain(3)
+
+        idle_bank = psum.tile([P, P], F32, tag="bank")
+        for turn_no in range(IDLE_TURNS):
+            nc.tensor.matmul(idle_bank[:], lhsT=ident_f32[:], rhs=ident_f32[:], start=True, stop=True)
 
         def turn_xn(j):
             bank = turn([xn[:, j, :]])
             group(xn_mx, j * P, bank, 1)
 
+        o_accs = {}
+
+        def second_multiply(j):
+            quantise(xn_mx, j * P, P)
+            o_accs[j] = multiply(xn_mx, j, wf_mx)
+
         def finish(j):
-            nc.vector.tensor_tensor(out=biased[:, j, :], in0=o_accs[j][:], in1=b_ffn_all[:], op=ALU.add)
+            nc.vector.tensor_tensor(
+                out=biased[:, j, :], in0=o_accs[j][:], in1=b_ffn_rows[:, 0, :], op=ALU.add
+            )
             nc.scalar.activation(out=result[:, j, :], in_=biased[:, j, :], func=ACT.Relu)
             nc.sync.dma_start(out=out_view[:, j, :], in_=result[:, j, :])
 
-        o_accs = []
-        normalise(0)
-        turn_xn(0)
         normalise(1)
         turn_xn(1)
-        quantise(wf_mx, 0, ROWS)
-        quantise(xn_mx, 0, P)
-        o_accs.append(multiply(xn_mx, 0, wf_mx))
         normalise(2)
         turn_xn(2)
-        quantise(xn_mx, P, P)
-        o_accs.append(multiply(xn_mx, 1, wf_mx))
+        quantise(wf_mx, 0, ROWS)
+        second_multiply(1)
+        turn_xn(0)
         normalise(3)
         turn_xn(3)
-        finish(0)
-        quantise(xn_mx, 2 * P, P)
-        o_accs.append(multiply(xn_mx, 2, wf_mx))
+        second_multiply(2)
         finish(1)
-        quantise(xn_mx, 3 * P, P)
-        o_accs.append(multiply(xn_mx, 3, wf_mx))
+        second_multiply(0)
         finish(2)
+        second_multiply(3)
+        finish(0)
         finish(3)

@@ -35,39 +35,40 @@ def tile_l1regressionmoeactionhead_pc_s_kernel(
         h_view = h_attn.flatten_outer_dims().rearrange("(p j) k -> p j k", j=ROW_TILES)
         x_view = x.flatten_outer_dims().rearrange("(p j) o -> p j o", j=ROW_TILES)
         out_view = out.flatten_outer_dims().rearrange("(p j) f -> p j f", j=ROW_TILES)
-        wo_view = W_o.rearrange("(j p) k -> p j k", p=P)
-        wf_view = W_ffn.rearrange("(j p) k -> p j k", p=P)
+        wo_view = W_o.rearrange("(p j) k -> p j k", j=ROW_TILES)
+        wf_view = W_ffn.rearrange("(p j) k -> p j k", j=ROW_TILES)
 
         def load_half(sb, view, half):
             tiles = slice(half * HALF_TILES, (half + 1) * HALF_TILES)
             nc.sync.dma_start(out=sb[:, tiles, :], in_=view[:, tiles, :])
 
-        def load_vec(vec, name):
-            cols = keep.tile([P, PACK], BF16, name=name)
-            nc.sync.dma_start(out=cols[:], in_=vec.rearrange("(q t) -> q t", t=PACK))
-            return cols
+        b_o_rows = keep.tile([P, DIM], BF16)
+        nc.vector.memset(b_o_rows[:].bitcast(F32), 0.0)
+        vec_rows = keep.tile([P, DIM // 2], BF16)
+        nc.vector.memset(vec_rows[:].bitcast(F32), 0.0)
+        ones = keep.tile([P, P], BF16)
+        nc.vector.memset(ones[:], 1.0)
 
         wo_sb = keep.tile([P, ROW_TILES, DIM], BF16)
         h_sb = keep.tile([P, ROW_TILES, DIM], BF16)
         x_sb = keep.tile([P, ROW_TILES, DIM], BF16)
         wf_sb = keep.tile([P, ROW_TILES, DIM], BF16)
-        b_o_cols = load_vec(b_o, "b_o_cols")
-        gamma_cols = load_vec(gamma, "gamma_cols")
-        beta_cols = load_vec(beta, "beta_cols")
         load_half(x_sb, x_view, 0)
+        nc.sync.dma_start(out=b_o_rows[0:1, :], in_=b_o.rearrange("(u c) -> u c", u=1))
+        for v, vec in enumerate((gamma, beta, b_ffn)):
+            nc.sync.dma_start(
+                out=vec_rows[2 * v : 2 * (v + 1), :], in_=vec.rearrange("(u c) -> u c", u=2)
+            )
         load_half(wo_sb, wo_view, 0)
         load_half(x_sb, x_view, 1)
         load_half(wo_sb, wo_view, 1)
         load_half(h_sb, h_view, 0)
         load_half(h_sb, h_view, 1)
-        b_ffn_cols = load_vec(b_ffn, "b_ffn_cols")
         load_half(wf_sb, wf_view, 0)
         load_half(wf_sb, wf_view, 1)
 
         ident_f32 = keep.tile([P, P], F32)
         make_identity(nc, ident_f32[:])
-        ident_bf16 = keep.tile([P, P], BF16)
-        nc.vector.tensor_copy(out=ident_bf16[:], in_=ident_f32[:])
         eps = keep.tile([P, 1], F32)
         nc.vector.memset(eps[:], EPS)
         warm = keep.tile([P, 1], F32)
@@ -119,25 +120,24 @@ def tile_l1regressionmoeactionhead_pc_s_kernel(
             )
             return acc
 
-        def spread(vecs):
-            bank = psum.tile([P, len(vecs), PACK, P], BF16, tag="bank")
-            for v, cols in enumerate(vecs):
-                for t in range(PACK):
+        def spread(first, n):
+            bank = psum.tile([P, n, 2, P], F32, tag="bank")
+            for i in range(n):
+                for u in range(2):
+                    col = 2 * (first + i) + u
                     nc.tensor.transpose(
-                        bank[:, v, t, :], cols[:, t : t + 1].to_broadcast([P, P]), ident_bf16[:]
+                        bank[:, i, u, :], vec_cols[:, col : col + 1].to_broadcast([P, P]), ident_f32[:]
                     )
             return bank
 
-        def in_order(bank, v):
-            return bank[:, v].rearrange("p t q -> p q t")
-
-        def by_fours(ap):
-            return ap.rearrange("p (q t) -> p q t", t=PACK)
+        def values(bank, v):
+            return bank[:, v].rearrange("p u c -> p (u c)").bitcast(BF16)
 
         def to_sbuf(bank, n, name):
             rows = keep.tile([P, n, DIM], BF16, name=name)
             nc.scalar.copy(
-                out=rows[:].rearrange("p v (q t) -> p v q t", t=PACK), in_=bank[:].rearrange("p v t q -> p v q t")
+                out=rows[:].bitcast(F32).rearrange("p v w -> p (v w)"),
+                in_=bank[:].rearrange("p v u c -> p (v u c)"),
             )
             return rows
 
@@ -158,12 +158,15 @@ def tile_l1regressionmoeactionhead_pc_s_kernel(
         biased = keep.tile([P, ROW_TILES, DIM], F32)
         result = keep.tile([P, ROW_TILES, DIM], F32)
 
-        b_o_bank = spread([b_o_cols])
-        gain_bank = spread([gamma_cols, beta_cols])
+        b_o_bank = psum.tile([P, DIM], F32, tag="bank")
+        nc.tensor.matmul(b_o_bank[:], lhsT=ones[:], rhs=b_o_rows[:], start=True, stop=True)
+        vec_bank = psum.tile([P, P], F32, tag="bank")
+        nc.tensor.transpose(vec_bank[:], vec_rows[:].bitcast(F32), ident_f32[:])
+        vec_cols = keep.tile([P, 6], F32)
+        nc.scalar.copy(out=vec_cols[:], in_=vec_bank[:, 0:6])
         for j in range(ROW_TILES):
             nc.vector.tensor_tensor(
-                out=by_fours(xb[:, j, :]), in0=by_fours(x_sb[:, j, :]), in1=in_order(b_o_bank, 0),
-                op=ALU.add,
+                out=xb[:, j, :], in0=x_sb[:, j, :], in1=b_o_bank[:], op=ALU.add
             )
         for half in range(2):
             first = half * HALF_TILES
@@ -176,13 +179,20 @@ def tile_l1regressionmoeactionhead_pc_s_kernel(
             group(h_mx, j * P, bank, 1)
         for j in range(ROW_TILES):
             quantise(h_mx, j * P, P)
-        accs = [multiply(h_mx, j, wo_mx) for j in range(ROW_TILES)]
+        gain_bank = spread(0, 2)
         gain_rows = to_sbuf(gain_bank, 2, "gain_rows")
-        b_ffn_bank = spread([b_ffn_cols])
+        accs = [multiply(h_mx, j, wo_mx) for j in range(ROW_TILES)]
+        b_ffn_bank = spread(2, 1)
+
+        def by_feature(ap):
+            return ap.rearrange("p (f j) -> p f j", j=ROW_TILES)
+
+        def from_product(acc):
+            return acc[:].rearrange("p (j f) -> p f j", j=ROW_TILES)
 
         def residual(j):
             nc.vector.scalar_tensor_tensor(
-                out=y[:, j, :], in0=accs[j][:], scalar=0.0, in1=xb[:, j, :],
+                out=by_feature(y[:, j, :]), in0=from_product(accs[j]), scalar=0.0, in1=by_feature(xb[:, j, :]),
                 op0=ALU.add, op1=ALU.add, accum_out=y_sum[:, j : j + 1],
             )
             nc.scalar.activation(
@@ -203,14 +213,14 @@ def tile_l1regressionmoeactionhead_pc_s_kernel(
 
         def gain(j):
             nc.vector.scalar_tensor_tensor(
-                out=by_fours(gained[:, j, :]), in0=by_fours(y[:, j, :]),
-                scalar=neg_mean[:, j : j + 1], in1=in_order(gain_bank, 0), op0=ALU.add, op1=ALU.mult,
+                out=gained[:, j, :], in0=y[:, j, :],
+                scalar=neg_mean[:, j : j + 1], in1=values(gain_bank, 0), op0=ALU.add, op1=ALU.mult,
             )
 
         def normalise(j):
             nc.vector.scalar_tensor_tensor(
-                out=by_fours(xn[:, j, :]), in0=by_fours(gained[:, j, :]),
-                scalar=rstd[:, j : j + 1], in1=in_order(gain_bank, 1), op0=ALU.mult, op1=ALU.add,
+                out=xn[:, j, :], in0=gained[:, j, :],
+                scalar=rstd[:, j : j + 1], in1=values(gain_bank, 1), op0=ALU.mult, op1=ALU.add,
             )
 
         residual(0)
@@ -256,7 +266,8 @@ def tile_l1regressionmoeactionhead_pc_s_kernel(
 
         def finish(j):
             nc.vector.tensor_tensor(
-                out=biased[:, j, :], in0=o_accs[j][:], in1=b_ffn_rows[:, 0, :], op=ALU.add
+                out=by_feature(biased[:, j, :]), in0=from_product(o_accs[j]), in1=by_feature(b_ffn_rows[:, 0, :]),
+                op=ALU.add,
             )
             nc.scalar.activation(out=result[:, j, :], in_=biased[:, j, :], func=ACT.Relu)
             nc.sync.dma_start(out=out_view[:, j, :], in_=result[:, j, :])

@@ -18,7 +18,6 @@ ROW_TILES = ROWS // P
 PACK = 4
 HALF_TILES = 2
 EPS = 1e-5
-IDLE_TURNS = 6
 
 FLOPS = 2 * 2 * ROWS * DIM * DIM
 
@@ -29,7 +28,7 @@ def tile_l1regressionmoeactionhead_pc_s_kernel(
     nc = tc.nc
     with ExitStack() as ctx:
         keep = ctx.enter_context(tc.tile_pool(name="keep", bufs=1))
-        psum = ctx.enter_context(tc.psum_pool(name="psum", bufs=8))
+        psum = ctx.enter_context(tc.psum_pool(name="psum", bufs=7))
         ctx.enter_context(tc.manual_schedule())
 
         h_view = h_attn.flatten_outer_dims().rearrange("(p j) k -> p j k", j=ROW_TILES)
@@ -42,23 +41,32 @@ def tile_l1regressionmoeactionhead_pc_s_kernel(
             tiles = slice(half * HALF_TILES, (half + 1) * HALF_TILES)
             nc.sync.dma_start(out=sb[:, tiles, :], in_=view[:, tiles, :])
 
-        b_o_rows = keep.tile([P, DIM], BF16)
-        nc.vector.memset(b_o_rows[:].bitcast(F32), 0.0)
-        vec_rows = keep.tile([P, DIM // 2], BF16)
-        nc.vector.memset(vec_rows[:].bitcast(F32), 0.0)
-        ones = keep.tile([P, P], BF16)
+        eps = keep.tile([P, 1], F32)
+        nc.vector.memset(eps[:], EPS)
+        def zero_rows(name):
+            rows = keep.tile([P, DIM // 2], BF16, name=name)
+            nc.gpsimd.memset(rows[:].bitcast(F32), 0.0)
+            return rows
+
+        def load_vec(rows, v, vec):
+            nc.scalar.dma_start(out=rows[2 * v : 2 * (v + 1), :], in_=vec.rearrange("(u c) -> u c", u=2))
+
+        vec_rows = zero_rows("vec_rows")
+        b_o_row = keep.tile([P, DIM], BF16)
+        nc.vector.memset(b_o_row[:].bitcast(F32), 0.0)
+        ones = keep.tile([P, P], F32)
         nc.vector.memset(ones[:], 1.0)
+        ones_bf16 = keep.tile([P, P], BF16)
+        nc.vector.memset(ones_bf16[:], 1.0)
 
         wo_sb = keep.tile([P, ROW_TILES, DIM], BF16)
         h_sb = keep.tile([P, ROW_TILES, DIM], BF16)
         x_sb = keep.tile([P, ROW_TILES, DIM], BF16)
         wf_sb = keep.tile([P, ROW_TILES, DIM], BF16)
         load_half(x_sb, x_view, 0)
-        nc.sync.dma_start(out=b_o_rows[0:1, :], in_=b_o.rearrange("(u c) -> u c", u=1))
+        nc.sync.dma_start(out=b_o_row[0:1, :], in_=b_o.rearrange("(u c) -> u c", u=1))
         for v, vec in enumerate((gamma, beta, b_ffn)):
-            nc.sync.dma_start(
-                out=vec_rows[2 * v : 2 * (v + 1), :], in_=vec.rearrange("(u c) -> u c", u=2)
-            )
+            load_vec(vec_rows, v, vec)
         load_half(wo_sb, wo_view, 0)
         load_half(x_sb, x_view, 1)
         load_half(wo_sb, wo_view, 1)
@@ -69,8 +77,6 @@ def tile_l1regressionmoeactionhead_pc_s_kernel(
 
         ident_f32 = keep.tile([P, P], F32)
         make_identity(nc, ident_f32[:])
-        eps = keep.tile([P, 1], F32)
-        nc.vector.memset(eps[:], EPS)
         warm = keep.tile([P, 1], F32)
         nc.scalar.activation(out=warm[:], in_=eps[:], func=ACT.Abs_reciprocal_sqrt)
 
@@ -120,15 +126,28 @@ def tile_l1regressionmoeactionhead_pc_s_kernel(
             )
             return acc
 
-        def spread(first, n):
+        def columns(rows, n, name):
+            bank = psum.tile([P, P], F32, tag="bank")
+            nc.tensor.transpose(bank[:], rows[:].bitcast(F32), ident_f32[:])
+            cols = keep.tile([P, 2 * n], F32, name=name)
+            nc.scalar.copy(out=cols[:], in_=bank[:, 0 : 2 * n])
+            return cols
+
+        def spread(cols, first, n):
             bank = psum.tile([P, n, 2, P], F32, tag="bank")
             for i in range(n):
                 for u in range(2):
                     col = 2 * (first + i) + u
                     nc.tensor.transpose(
-                        bank[:, i, u, :], vec_cols[:, col : col + 1].to_broadcast([P, P]), ident_f32[:]
+                        bank[:, i, u, :], cols[:, col : col + 1].to_broadcast([P, P]), ident_f32[:]
                     )
             return bank
+
+        busy_bank = psum.tile([P, P], F32, tag="busy", bufs=1)
+
+        def stay_awake(n, rhs):
+            for i in range(n):
+                nc.tensor.matmul(busy_bank[:], lhsT=ones[:], rhs=rhs, start=True, stop=True)
 
         def values(bank, v):
             return bank[:, v].rearrange("p u c -> p (u c)").bitcast(BF16)
@@ -158,12 +177,10 @@ def tile_l1regressionmoeactionhead_pc_s_kernel(
         biased = keep.tile([P, ROW_TILES, DIM], F32)
         result = keep.tile([P, ROW_TILES, DIM], F32)
 
+        stay_awake(2, ones[:])
         b_o_bank = psum.tile([P, DIM], F32, tag="bank")
-        nc.tensor.matmul(b_o_bank[:], lhsT=ones[:], rhs=b_o_rows[:], start=True, stop=True)
-        vec_bank = psum.tile([P, P], F32, tag="bank")
-        nc.tensor.transpose(vec_bank[:], vec_rows[:].bitcast(F32), ident_f32[:])
-        vec_cols = keep.tile([P, 6], F32)
-        nc.scalar.copy(out=vec_cols[:], in_=vec_bank[:, 0:6])
+        nc.tensor.matmul(b_o_bank[:], lhsT=ones_bf16[:], rhs=b_o_row[:], start=True, stop=True)
+        vec_cols = columns(vec_rows, 3, "vec_cols")
         for j in range(ROW_TILES):
             nc.vector.tensor_tensor(
                 out=xb[:, j, :], in0=x_sb[:, j, :], in1=b_o_bank[:], op=ALU.add
@@ -172,6 +189,8 @@ def tile_l1regressionmoeactionhead_pc_s_kernel(
             first = half * HALF_TILES
             bank = turn([wo_sb[:, first + i, :] for i in range(HALF_TILES)])
             group(wo_mx, first * P, bank, HALF_TILES)
+            if half == 1:
+                stay_awake(1, ones[:])
         for half in range(2):
             quantise(wo_mx, half * HALF_TILES * P, HALF_TILES * P)
         for j in range(ROW_TILES):
@@ -179,10 +198,10 @@ def tile_l1regressionmoeactionhead_pc_s_kernel(
             group(h_mx, j * P, bank, 1)
         for j in range(ROW_TILES):
             quantise(h_mx, j * P, P)
-        gain_bank = spread(0, 2)
+        gain_bank = spread(vec_cols, 0, 2)
         gain_rows = to_sbuf(gain_bank, 2, "gain_rows")
         accs = [multiply(h_mx, j, wo_mx) for j in range(ROW_TILES)]
-        b_ffn_bank = spread(2, 1)
+        b_ffn_bank = spread(vec_cols, 2, 1)
 
         def by_feature(ap):
             return ap.rearrange("p (f j) -> p f j", j=ROW_TILES)
@@ -242,17 +261,15 @@ def tile_l1regressionmoeactionhead_pc_s_kernel(
         nc.gpsimd.tensor_tensor(out=scaled[:], in0=centred[:], in1=gain_rows[:, 0, :], op=ALU.mult)
         nc.gpsimd.tensor_tensor(out=xn[:, 0, :], in0=scaled[:], in1=gain_rows[:, 1, :], op=ALU.add)
 
-        gain(2)
         for half in range(2):
             first = half * HALF_TILES
             bank = turn([wf_sb[:, first + i, :] for i in range(HALF_TILES)])
             group(wf_mx, first * P, bank, HALF_TILES)
         b_ffn_rows = to_sbuf(b_ffn_bank, 1, "b_ffn_rows")
+        gain(2)
         gain(3)
-
-        idle_bank = psum.tile([P, P], F32, tag="bank")
-        for turn_no in range(IDLE_TURNS):
-            nc.tensor.matmul(idle_bank[:], lhsT=ident_f32[:], rhs=ident_f32[:], start=True, stop=True)
+        for j in range(1, ROW_TILES):
+            stay_awake(1, gained[:, j, 0:P])
 
         def turn_xn(j):
             bank = turn([xn[:, j, :]])
@@ -274,6 +291,7 @@ def tile_l1regressionmoeactionhead_pc_s_kernel(
 
         normalise(1)
         turn_xn(1)
+        stay_awake(1, ones[:])
         normalise(2)
         turn_xn(2)
         quantise(wf_mx, 0, ROWS)

@@ -178,19 +178,19 @@ def tile_l1regressionmoeactionhead_pc_s_kernel(
         result = keep.tile([P, ROW_TILES, DIM], F32)
 
         stay_awake(2, ones[:])
-        b_o_bank = psum.tile([P, DIM], F32, tag="bank")
-        nc.tensor.matmul(b_o_bank[:], lhsT=ones_bf16[:], rhs=b_o_row[:], start=True, stop=True)
+        b_o_bank = psum.tile([P, 1, DIM], F32, tag="bank")
+        nc.tensor.matmul(b_o_bank[:, 0, :], lhsT=ones_bf16[:], rhs=b_o_row[:], start=True, stop=True)
         vec_cols = columns(vec_rows, 3, "vec_cols")
-        for j in range(ROW_TILES):
+        for half in range(2):
+            tiles = slice(half * HALF_TILES, (half + 1) * HALF_TILES)
             nc.vector.tensor_tensor(
-                out=xb[:, j, :], in0=x_sb[:, j, :], in1=b_o_bank[:], op=ALU.add
+                out=xb[:, tiles, :], in0=x_sb[:, tiles, :],
+                in1=b_o_bank[:].to_broadcast([P, HALF_TILES, DIM]), op=ALU.add,
             )
         for half in range(2):
             first = half * HALF_TILES
             bank = turn([wo_sb[:, first + i, :] for i in range(HALF_TILES)])
             group(wo_mx, first * P, bank, HALF_TILES)
-            if half == 1:
-                stay_awake(1, ones[:])
         for half in range(2):
             quantise(wo_mx, half * HALF_TILES * P, HALF_TILES * P)
         for j in range(ROW_TILES):
@@ -265,10 +265,11 @@ def tile_l1regressionmoeactionhead_pc_s_kernel(
             first = half * HALF_TILES
             bank = turn([wf_sb[:, first + i, :] for i in range(HALF_TILES)])
             group(wf_mx, first * P, bank, HALF_TILES)
+        stay_awake(1, ones[:])
         b_ffn_rows = to_sbuf(b_ffn_bank, 1, "b_ffn_rows")
         gain(2)
         gain(3)
-        for j in range(1, ROW_TILES):
+        for j in range(1, ROW_TILES - 1):
             stay_awake(1, gained[:, j, 0:P])
 
         def turn_xn(j):
@@ -281,17 +282,23 @@ def tile_l1regressionmoeactionhead_pc_s_kernel(
             quantise(xn_mx, j * P, P)
             o_accs[j] = multiply(xn_mx, j, wf_mx)
 
-        def finish(j):
-            nc.vector.tensor_tensor(
-                out=by_feature(biased[:, j, :]), in0=from_product(o_accs[j]), in1=by_feature(b_ffn_rows[:, 0, :]),
-                op=ALU.add,
-            )
-            nc.scalar.activation(out=result[:, j, :], in_=biased[:, j, :], func=ACT.Relu)
-            nc.sync.dma_start(out=out_view[:, j, :], in_=result[:, j, :])
+        def finish(j, pieces=1):
+            width = DIM // pieces
+            for i in range(pieces):
+                cols = slice(i * width, (i + 1) * width)
+                runs = slice(i * width // ROW_TILES, (i + 1) * width // ROW_TILES)
+                nc.vector.tensor_tensor(
+                    out=by_feature(biased[:, j, cols]), in0=from_product(o_accs[j])[:, runs, :],
+                    in1=by_feature(b_ffn_rows[:, 0, cols]), op=ALU.add,
+                )
+                if i == 1:
+                    nc.vector.tensor_scalar_max(out=result[:, j, cols], in0=biased[:, j, cols], scalar1=0.0)
+                else:
+                    nc.scalar.activation(out=result[:, j, cols], in_=biased[:, j, cols], func=ACT.Relu)
+                nc.sync.dma_start(out=out_view[:, j, cols], in_=result[:, j, cols])
 
         normalise(1)
         turn_xn(1)
-        stay_awake(1, ones[:])
         normalise(2)
         turn_xn(2)
         quantise(wf_mx, 0, ROWS)
@@ -305,4 +312,4 @@ def tile_l1regressionmoeactionhead_pc_s_kernel(
         finish(2)
         second_multiply(3)
         finish(0)
-        finish(3)
+        finish(3, pieces=2)

@@ -191,6 +191,8 @@ def tile_l1regressionmoeactionhead_pc_s_kernel(
             first = half * HALF_TILES
             bank = turn([wo_sb[:, first + i, :] for i in range(HALF_TILES)])
             group(wo_mx, first * P, bank, HALF_TILES)
+            if half == 0:
+                gain_bank = spread(vec_cols, 0, 2)
         for half in range(2):
             quantise(wo_mx, half * HALF_TILES * P, HALF_TILES * P)
         for j in range(ROW_TILES):
@@ -198,7 +200,6 @@ def tile_l1regressionmoeactionhead_pc_s_kernel(
             group(h_mx, j * P, bank, 1)
         for j in range(ROW_TILES):
             quantise(h_mx, j * P, P)
-        gain_bank = spread(vec_cols, 0, 2)
         gain_rows = to_sbuf(gain_bank, 2, "gain_rows")
         accs = [multiply(h_mx, j, wo_mx) for j in range(ROW_TILES)]
         b_ffn_bank = spread(vec_cols, 2, 1)
@@ -282,20 +283,16 @@ def tile_l1regressionmoeactionhead_pc_s_kernel(
             quantise(xn_mx, j * P, P)
             o_accs[j] = multiply(xn_mx, j, wf_mx)
 
-        def finish(j, pieces=1):
-            width = DIM // pieces
-            for i in range(pieces):
-                cols = slice(i * width, (i + 1) * width)
-                runs = slice(i * width // ROW_TILES, (i + 1) * width // ROW_TILES)
-                nc.vector.tensor_tensor(
-                    out=by_feature(biased[:, j, cols]), in0=from_product(o_accs[j])[:, runs, :],
-                    in1=by_feature(b_ffn_rows[:, 0, cols]), op=ALU.add,
-                )
-                if i == 1:
-                    nc.vector.tensor_scalar_max(out=result[:, j, cols], in0=biased[:, j, cols], scalar1=0.0)
-                else:
-                    nc.scalar.activation(out=result[:, j, cols], in_=biased[:, j, cols], func=ACT.Relu)
-                nc.sync.dma_start(out=out_view[:, j, cols], in_=result[:, j, cols])
+        def finish(j, rectifier=nc.scalar):
+            nc.vector.tensor_tensor(
+                out=by_feature(biased[:, j, :]), in0=from_product(o_accs[j]), in1=by_feature(b_ffn_rows[:, 0, :]),
+                op=ALU.add,
+            )
+            if rectifier is nc.scalar:
+                nc.scalar.activation(out=result[:, j, :], in_=biased[:, j, :], func=ACT.Relu)
+            else:
+                nc.vector.tensor_scalar_max(out=result[:, j, :], in0=biased[:, j, :], scalar1=0.0)
+            nc.sync.dma_start(out=out_view[:, j, :], in_=result[:, j, :])
 
         normalise(1)
         turn_xn(1)
@@ -312,4 +309,4 @@ def tile_l1regressionmoeactionhead_pc_s_kernel(
         finish(2)
         second_multiply(3)
         finish(0)
-        finish(3, pieces=2)
+        finish(3, rectifier=nc.vector)

@@ -193,6 +193,7 @@ def tile_l1regressionmoeactionhead_pc_s_kernel(
             group(wo_mx, first * P, bank, HALF_TILES)
             if half == 0:
                 gain_bank = spread(vec_cols, 0, 2)
+                stay_awake(1, ones[:])
         for half in range(2):
             quantise(wo_mx, half * HALF_TILES * P, HALF_TILES * P)
         for j in range(ROW_TILES):
@@ -270,7 +271,7 @@ def tile_l1regressionmoeactionhead_pc_s_kernel(
         b_ffn_rows = to_sbuf(b_ffn_bank, 1, "b_ffn_rows")
         gain(2)
         gain(3)
-        for j in range(1, ROW_TILES - 1):
+        for j in range(1, ROW_TILES):
             stay_awake(1, gained[:, j, 0:P])
 
         def turn_xn(j):
@@ -296,6 +297,7 @@ def tile_l1regressionmoeactionhead_pc_s_kernel(
 
         normalise(1)
         turn_xn(1)
+        stay_awake(1, ones[:])
         normalise(2)
         turn_xn(2)
         quantise(wf_mx, 0, ROWS)

@@ -267,7 +267,6 @@ def tile_l1regressionmoeactionhead_pc_s_kernel(
             first = half * HALF_TILES
             bank = turn([wf_sb[:, first + i, :] for i in range(HALF_TILES)])
             group(wf_mx, first * P, bank, HALF_TILES)
-        stay_awake(1, ones[:])
         b_ffn_rows = to_sbuf(b_ffn_bank, 1, "b_ffn_rows")
         gain(2)
         gain(3)
@@ -300,6 +299,7 @@ def tile_l1regressionmoeactionhead_pc_s_kernel(
         stay_awake(1, ones[:])
         normalise(2)
         turn_xn(2)
+        stay_awake(1, ones[:])
         quantise(wf_mx, 0, ROWS)
         second_multiply(1)
         turn_xn(0)

@@ -43,15 +43,11 @@ def tile_l1regressionmoeactionhead_pc_s_kernel(
 
         eps = keep.tile([P, 1], F32)
         nc.vector.memset(eps[:], EPS)
-        def zero_rows(name):
-            rows = keep.tile([P, DIM // 2], BF16, name=name)
-            nc.gpsimd.memset(rows[:].bitcast(F32), 0.0)
-            return rows
+        def load_row(queue, rows, v, vec):
+            queue.dma_start(out=rows[v : v + 1, :], in_=vec.rearrange("(u c) -> u c", u=1))
 
-        def load_vec(rows, v, vec):
-            nc.scalar.dma_start(out=rows[2 * v : 2 * (v + 1), :], in_=vec.rearrange("(u c) -> u c", u=2))
-
-        vec_rows = zero_rows("vec_rows")
+        vec_rows = keep.tile([P, DIM], BF16)
+        nc.gpsimd.memset(vec_rows[:].bitcast(F32), 0.0)
         b_o_row = keep.tile([P, DIM], BF16)
         nc.vector.memset(b_o_row[:].bitcast(F32), 0.0)
         ones = keep.tile([P, P], F32)
@@ -64,9 +60,9 @@ def tile_l1regressionmoeactionhead_pc_s_kernel(
         x_sb = keep.tile([P, ROW_TILES, DIM], BF16)
         wf_sb = keep.tile([P, ROW_TILES, DIM], BF16)
         load_half(x_sb, x_view, 0)
-        nc.sync.dma_start(out=b_o_row[0:1, :], in_=b_o.rearrange("(u c) -> u c", u=1))
+        load_row(nc.sync, b_o_row, 0, b_o)
         for v, vec in enumerate((gamma, beta, b_ffn)):
-            load_vec(vec_rows, v, vec)
+            load_row(nc.scalar, vec_rows, v, vec)
         load_half(wo_sb, wo_view, 0)
         load_half(x_sb, x_view, 1)
         load_half(wo_sb, wo_view, 1)
@@ -86,21 +82,38 @@ def tile_l1regressionmoeactionhead_pc_s_kernel(
             scales = keep.tile([P, ROWS], U8, align_bytes=64, name=name + "_scales")
             return grouped, codes, scales
 
-        def turn(row_tiles):
+        def turn(row_tiles, side_by_side=False):
             n = len(row_tiles)
             bank = psum.tile([P, n, 2, P], F32, tag="bank")
             for i, rows in enumerate(row_tiles):
                 words = rows.bitcast(F32)
                 for u in range(2):
-                    nc.tensor.transpose(bank[:, i, u, :], words[:, u : 2 * P : 2], ident_f32[:])
+                    picked = words[:, u * P : (u + 1) * P] if side_by_side else words[:, u : 2 * P : 2]
+                    nc.tensor.transpose(bank[:, i, u, :], picked, ident_f32[:])
             return bank
 
-        def group(operand, first_col, bank, n):
+        def words_of(operand):
+            return operand[0][:].bitcast(F32)
+
+        def group_tile(operand, j, bank):
             nc.scalar.copy(
-                out=operand[0][:].bitcast(F32)[:, first_col : first_col + n * P, :].rearrange(
-                    "p (i r) u -> p i r u", i=n
+                out=words_of(operand)[:, j * P : (j + 1) * P, :],
+                in_=bank[:, 0].rearrange("p u r -> p r u"),
+            )
+
+        def group_wo(half, bank):
+            nc.scalar.copy(
+                out=words_of(wo_mx)[:, half * 2 * P : (half + 1) * 2 * P, :].rearrange(
+                    "p (r i) u -> p r i u", i=HALF_TILES
                 ),
-                in_=bank[:].rearrange("p i u r -> p i r u"),
+                in_=bank[:].rearrange("p i u r -> p r i u"),
+            )
+
+        def group_wf(half, bank):
+            tiles = slice(half * HALF_TILES, (half + 1) * HALF_TILES)
+            nc.scalar.copy(
+                out=words_of(wf_mx).rearrange("p (r j) u -> p r j u", j=ROW_TILES)[:, :, tiles, :],
+                in_=bank[:].rearrange("p i u r -> p r i u"),
             )
 
         def quantise(operand, first_col, n_cols):
@@ -127,19 +140,21 @@ def tile_l1regressionmoeactionhead_pc_s_kernel(
             return acc
 
         def columns(rows, n, name):
-            bank = psum.tile([P, P], F32, tag="bank")
-            nc.tensor.transpose(bank[:], rows[:].bitcast(F32), ident_f32[:])
-            cols = keep.tile([P, 2 * n], F32, name=name)
-            nc.scalar.copy(out=cols[:], in_=bank[:, 0 : 2 * n])
+            bank = psum.tile([P, 2, P], F32, tag="bank")
+            for u in range(2):
+                nc.tensor.transpose(bank[:, u, :], rows[:].bitcast(F32)[:, u:DIM // 2:2], ident_f32[:])
+            cols = keep.tile([P, 2, n], F32, name=name)
+            nc.scalar.copy(out=cols[:], in_=bank[:, :, 0:n])
             return cols
 
         def spread(cols, first, n):
             bank = psum.tile([P, n, 2, P], F32, tag="bank")
             for i in range(n):
                 for u in range(2):
-                    col = 2 * (first + i) + u
                     nc.tensor.transpose(
-                        bank[:, i, u, :], cols[:, col : col + 1].to_broadcast([P, P]), ident_f32[:]
+                        bank[:, i, u, :],
+                        cols[:, u, first + i : first + i + 1].to_broadcast([P, P]),
+                        ident_f32[:],
                     )
             return bank
 
@@ -151,14 +166,6 @@ def tile_l1regressionmoeactionhead_pc_s_kernel(
 
         def values(bank, v):
             return bank[:, v].rearrange("p u c -> p (u c)").bitcast(BF16)
-
-        def to_sbuf(bank, n, name):
-            rows = keep.tile([P, n, DIM], BF16, name=name)
-            nc.scalar.copy(
-                out=rows[:].bitcast(F32).rearrange("p v w -> p (v w)"),
-                in_=bank[:].rearrange("p v u c -> p (v u c)"),
-            )
-            return rows
 
         wo_mx = mx_tiles("wo")
         h_mx = mx_tiles("h")
@@ -178,42 +185,37 @@ def tile_l1regressionmoeactionhead_pc_s_kernel(
         result = keep.tile([P, ROW_TILES, DIM], F32)
 
         stay_awake(2, ones[:])
-        b_o_bank = psum.tile([P, 1, DIM], F32, tag="bank")
-        nc.tensor.matmul(b_o_bank[:, 0, :], lhsT=ones_bf16[:], rhs=b_o_row[:], start=True, stop=True)
+        b_o_bank = psum.tile([P, DIM], F32, tag="bank")
+        nc.tensor.matmul(b_o_bank[:], lhsT=ones_bf16[:], rhs=b_o_row[:], start=True, stop=True)
         vec_cols = columns(vec_rows, 3, "vec_cols")
-        for half in range(2):
-            tiles = slice(half * HALF_TILES, (half + 1) * HALF_TILES)
+        for j in range(ROW_TILES):
             nc.vector.tensor_tensor(
-                out=xb[:, tiles, :], in0=x_sb[:, tiles, :],
-                in1=b_o_bank[:].to_broadcast([P, HALF_TILES, DIM]), op=ALU.add,
+                out=xb[:, j, :].rearrange("p (u q e) -> p u q e", u=2, e=2),
+                in0=x_sb[:, j, :].rearrange("p (q u e) -> p u q e", u=2, e=2),
+                in1=b_o_bank[:].rearrange("p (q u e) -> p u q e", u=2, e=2), op=ALU.add,
             )
         for half in range(2):
-            first = half * HALF_TILES
-            bank = turn([wo_sb[:, first + i, :] for i in range(HALF_TILES)])
-            group(wo_mx, first * P, bank, HALF_TILES)
+            group_wo(half, turn([wo_sb[:, half * HALF_TILES + i, :] for i in range(HALF_TILES)]))
             if half == 0:
                 gain_bank = spread(vec_cols, 0, 2)
                 stay_awake(1, ones[:])
         for half in range(2):
             quantise(wo_mx, half * HALF_TILES * P, HALF_TILES * P)
         for j in range(ROW_TILES):
-            bank = turn([h_sb[:, j, :]])
-            group(h_mx, j * P, bank, 1)
+            group_tile(h_mx, j, turn([h_sb[:, j, :]]))
         for j in range(ROW_TILES):
             quantise(h_mx, j * P, P)
-        gain_rows = to_sbuf(gain_bank, 2, "gain_rows")
+        gain_rows = keep.tile([P, 2, DIM], BF16)
+        nc.scalar.copy(
+            out=gain_rows[:].bitcast(F32).rearrange("p v w -> p (v w)"),
+            in_=gain_bank[:].rearrange("p v u q -> p (v u q)"),
+        )
         accs = [multiply(h_mx, j, wo_mx) for j in range(ROW_TILES)]
         b_ffn_bank = spread(vec_cols, 2, 1)
 
-        def by_feature(ap):
-            return ap.rearrange("p (f j) -> p f j", j=ROW_TILES)
-
-        def from_product(acc):
-            return acc[:].rearrange("p (j f) -> p f j", j=ROW_TILES)
-
         def residual(j):
             nc.vector.scalar_tensor_tensor(
-                out=by_feature(y[:, j, :]), in0=from_product(accs[j]), scalar=0.0, in1=by_feature(xb[:, j, :]),
+                out=y[:, j, :], in0=accs[j][:], scalar=0.0, in1=xb[:, j, :],
                 op0=ALU.add, op1=ALU.add, accum_out=y_sum[:, j : j + 1],
             )
             nc.scalar.activation(
@@ -264,18 +266,19 @@ def tile_l1regressionmoeactionhead_pc_s_kernel(
         nc.gpsimd.tensor_tensor(out=xn[:, 0, :], in0=scaled[:], in1=gain_rows[:, 1, :], op=ALU.add)
 
         for half in range(2):
-            first = half * HALF_TILES
-            bank = turn([wf_sb[:, first + i, :] for i in range(HALF_TILES)])
-            group(wf_mx, first * P, bank, HALF_TILES)
-        b_ffn_rows = to_sbuf(b_ffn_bank, 1, "b_ffn_rows")
+            group_wf(half, turn([wf_sb[:, half * HALF_TILES + i, :] for i in range(HALF_TILES)]))
+        b_ffn_row = keep.tile([P, DIM], BF16)
+        nc.scalar.copy(
+            out=b_ffn_row[:].bitcast(F32).rearrange("p (q u) -> p q u", u=2),
+            in_=b_ffn_bank[:, 0].rearrange("p u q -> p q u"),
+        )
         gain(2)
         gain(3)
         for j in range(1, ROW_TILES):
             stay_awake(1, gained[:, j, 0:P])
 
         def turn_xn(j):
-            bank = turn([xn[:, j, :]])
-            group(xn_mx, j * P, bank, 1)
+            group_tile(xn_mx, j, turn([xn[:, j, :]], side_by_side=True))
 
         o_accs = {}
 
@@ -284,14 +287,17 @@ def tile_l1regressionmoeactionhead_pc_s_kernel(
             o_accs[j] = multiply(xn_mx, j, wf_mx)
 
         def finish(j, rectifier=nc.scalar):
-            nc.vector.tensor_tensor(
-                out=by_feature(biased[:, j, :]), in0=from_product(o_accs[j]), in1=by_feature(b_ffn_rows[:, 0, :]),
-                op=ALU.add,
-            )
             if rectifier is nc.scalar:
+                nc.vector.tensor_tensor(out=biased[:, j, :], in0=o_accs[j][:], in1=b_ffn_row[:], op=ALU.add)
                 nc.scalar.activation(out=result[:, j, :], in_=biased[:, j, :], func=ACT.Relu)
             else:
-                nc.vector.tensor_scalar_max(out=result[:, j, :], in0=biased[:, j, :], scalar1=0.0)
+                halves = [slice(0, DIM // 2), slice(DIM // 2, DIM)]
+                for cols in halves:
+                    nc.vector.tensor_tensor(
+                        out=biased[:, j, cols], in0=o_accs[j][:, cols], in1=b_ffn_row[:, cols], op=ALU.add
+                    )
+                for cols in halves:
+                    nc.vector.tensor_scalar_max(out=result[:, j, cols], in0=biased[:, j, cols], scalar1=0.0)
             nc.sync.dma_start(out=out_view[:, j, :], in_=result[:, j, :])
 
         normalise(1)

@@ -59,13 +59,13 @@ def tile_l1regressionmoeactionhead_pc_s_kernel(
         h_sb = keep.tile([P, ROW_TILES, DIM], BF16)
         x_sb = keep.tile([P, ROW_TILES, DIM], BF16)
         wf_sb = keep.tile([P, ROW_TILES, DIM], BF16)
-        load_half(x_sb, x_view, 0)
+        load_half(wo_sb, wo_view, 0)
         load_row(nc.sync, b_o_row, 0, b_o)
         for v, vec in enumerate((gamma, beta, b_ffn)):
             load_row(nc.scalar, vec_rows, v, vec)
-        load_half(wo_sb, wo_view, 0)
-        load_half(x_sb, x_view, 1)
+        load_half(x_sb, x_view, 0)
         load_half(wo_sb, wo_view, 1)
+        load_half(x_sb, x_view, 1)
         load_half(h_sb, h_view, 0)
         load_half(h_sb, h_view, 1)
         load_half(wf_sb, wf_view, 0)
@@ -187,37 +187,48 @@ def tile_l1regressionmoeactionhead_pc_s_kernel(
         stay_awake(2, ones[:])
         b_o_bank = psum.tile([P, DIM], F32, tag="bank")
         nc.tensor.matmul(b_o_bank[:], lhsT=ones_bf16[:], rhs=b_o_row[:], start=True, stop=True)
-        vec_cols = columns(vec_rows, 3, "vec_cols")
-        for j in range(ROW_TILES):
+        def add_b_o(j):
             nc.vector.tensor_tensor(
                 out=xb[:, j, :].rearrange("p (u q e) -> p u q e", u=2, e=2),
                 in0=x_sb[:, j, :].rearrange("p (q u e) -> p u q e", u=2, e=2),
                 in1=b_o_bank[:].rearrange("p (q u e) -> p u q e", u=2, e=2), op=ALU.add,
             )
-        for half in range(2):
+
+        def turn_wo(half):
             group_wo(half, turn([wo_sb[:, half * HALF_TILES + i, :] for i in range(HALF_TILES)]))
-            if half == 0:
-                gain_bank = spread(vec_cols, 0, 2)
-                stay_awake(1, ones[:])
-        for half in range(2):
-            quantise(wo_mx, half * HALF_TILES * P, HALF_TILES * P)
-        for j in range(ROW_TILES):
+
+        def turn_wf(half):
+            group_wf(half, turn([wf_sb[:, half * HALF_TILES + i, :] for i in range(HALF_TILES)]))
+
+        def turn_h(j):
             group_tile(h_mx, j, turn([h_sb[:, j, :]]))
-        for j in range(ROW_TILES):
-            quantise(h_mx, j * P, P)
+
+        accs = {}
         gain_rows = keep.tile([P, 2, DIM], BF16)
-        nc.scalar.copy(
-            out=gain_rows[:].bitcast(F32).rearrange("p v w -> p (v w)"),
-            in_=gain_bank[:].rearrange("p v u q -> p (v u q)"),
-        )
-        accs = [multiply(h_mx, j, wo_mx) for j in range(ROW_TILES)]
-        b_ffn_bank = spread(vec_cols, 2, 1)
+        b_ffn_row = keep.tile([P, DIM], BF16)
+
+        def first_multiply(j):
+            accs[j] = multiply(h_mx, j, wo_mx)
+
+        def copy_gain():
+            nc.scalar.copy(
+                out=gain_rows[:].bitcast(F32).rearrange("p v w -> p (v w)"),
+                in_=gain_bank[:].rearrange("p v u q -> p (v u q)"),
+            )
+
+        def copy_b_ffn():
+            nc.scalar.copy(
+                out=b_ffn_row[:].bitcast(F32).rearrange("p (q u) -> p q u", u=2),
+                in_=b_ffn_bank[:, 0].rearrange("p u q -> p q u"),
+            )
 
         def residual(j):
             nc.vector.scalar_tensor_tensor(
                 out=y[:, j, :], in0=accs[j][:], scalar=0.0, in1=xb[:, j, :],
                 op0=ALU.add, op1=ALU.add, accum_out=y_sum[:, j : j + 1],
             )
+
+        def square(j):
             nc.scalar.activation(
                 out=squares[:, j, :], in_=y[:, j, :], func=ACT.Square,
                 bias=y_sum[:, j : j + 1], scale=-1.0 * DIM, accum_out=sq_sum[:, j : j + 1],
@@ -246,36 +257,16 @@ def tile_l1regressionmoeactionhead_pc_s_kernel(
                 scalar=rstd[:, j : j + 1], in1=values(gain_bank, 1), op0=ALU.mult, op1=ALU.add,
             )
 
-        residual(0)
-        residual(1)
-        spread_rstd(0, 2)
-        residual(2)
-        negate_mean(0, 2)
-        residual(3)
-        spread_rstd(2, 2)
-        gain(1)
-        negate_mean(2, 2)
+        def normalise_on_gpsimd(j):
+            nc.gpsimd.tensor_scalar(
+                out=centred[:], in0=y[:, j, :], scalar1=neg_mean[:, j : j + 1], scalar2=rstd[:, j : j + 1],
+                op0=ALU.add, op1=ALU.mult,
+            )
+            nc.gpsimd.tensor_tensor(out=scaled[:], in0=centred[:], in1=gain_rows[:, 0, :], op=ALU.mult)
+            nc.gpsimd.tensor_tensor(out=xn[:, j, :], in0=scaled[:], in1=gain_rows[:, 1, :], op=ALU.add)
 
         centred = keep.tile([P, DIM], F32)
         scaled = keep.tile([P, DIM], F32)
-        nc.gpsimd.tensor_scalar(
-            out=centred[:], in0=y[:, 0, :], scalar1=neg_mean[:, 0:1], scalar2=rstd[:, 0:1],
-            op0=ALU.add, op1=ALU.mult,
-        )
-        nc.gpsimd.tensor_tensor(out=scaled[:], in0=centred[:], in1=gain_rows[:, 0, :], op=ALU.mult)
-        nc.gpsimd.tensor_tensor(out=xn[:, 0, :], in0=scaled[:], in1=gain_rows[:, 1, :], op=ALU.add)
-
-        for half in range(2):
-            group_wf(half, turn([wf_sb[:, half * HALF_TILES + i, :] for i in range(HALF_TILES)]))
-        b_ffn_row = keep.tile([P, DIM], BF16)
-        nc.scalar.copy(
-            out=b_ffn_row[:].bitcast(F32).rearrange("p (q u) -> p q u", u=2),
-            in_=b_ffn_bank[:, 0].rearrange("p u q -> p q u"),
-        )
-        gain(2)
-        gain(3)
-        for j in range(1, ROW_TILES):
-            stay_awake(1, gained[:, j, 0:P])
 
         def turn_xn(j):
             group_tile(xn_mx, j, turn([xn[:, j, :]], side_by_side=True))
@@ -283,7 +274,6 @@ def tile_l1regressionmoeactionhead_pc_s_kernel(
         o_accs = {}
 
         def second_multiply(j):
-            quantise(xn_mx, j * P, P)
             o_accs[j] = multiply(xn_mx, j, wf_mx)
 
         def finish(j, rectifier=nc.scalar):
@@ -300,21 +290,74 @@ def tile_l1regressionmoeactionhead_pc_s_kernel(
                     nc.vector.tensor_scalar_max(out=result[:, j, cols], in0=biased[:, j, cols], scalar1=0.0)
             nc.sync.dma_start(out=out_view[:, j, :], in_=result[:, j, :])
 
-        normalise(1)
-        turn_xn(1)
+        turn_wo(0)
+        turn_wo(1)
+        vec_cols = columns(vec_rows, 3, "vec_cols")
         stay_awake(1, ones[:])
+        add_b_o(0)
+        add_b_o(1)
+        add_b_o(2)
+        turn_h(0)
+        turn_h(1)
+        quantise(wo_mx, 0, 2 * P)
+        quantise(wo_mx, 2 * P, 2 * P)
+        turn_h(2)
+        turn_h(3)
+        gain_bank = spread(vec_cols, 0, 2)
+        copy_gain()
+        stay_awake(1, ones[:])
+        b_ffn_bank = spread(vec_cols, 2, 1)
+        copy_b_ffn()
+        quantise(h_mx, 0, P)
+        add_b_o(3)
+        first_multiply(0)
+        quantise(h_mx, P, P)
+        first_multiply(1)
+        quantise(h_mx, 2 * P, P)
+        first_multiply(2)
+        residual(0)
+        square(0)
+        quantise(h_mx, 3 * P, P)
+        first_multiply(3)
+        residual(1)
+        square(1)
+        spread_rstd(0, 1)
+        residual(2)
+        square(2)
+        negate_mean(0, 2)
+        normalise_on_gpsimd(0)
+        spread_rstd(1, 1)
+        residual(3)
+        square(3)
+        gain(1)
+        negate_mean(2, 2)
+        normalise(1)
+        turn_wf(0)
+        spread_rstd(2, 2)
+        turn_wf(1)
+        stay_awake(1, gained[:, 1, 0:P])
+        turn_xn(1)
+        gain(2)
+        stay_awake(1, gained[:, 2, 0:P])
+        gain(3)
+        stay_awake(1, gained[:, 3, 0:P])
         normalise(2)
         turn_xn(2)
         stay_awake(1, ones[:])
-        quantise(wf_mx, 0, ROWS)
-        second_multiply(1)
-        turn_xn(0)
         normalise(3)
+        turn_xn(0)
         turn_xn(3)
+        quantise(wf_mx, 0, ROWS)
+        quantise(xn_mx, P, P)
+        second_multiply(1)
+        quantise(xn_mx, 2 * P, P)
         second_multiply(2)
-        finish(1)
+        quantise(xn_mx, 0, P)
         second_multiply(0)
-        finish(2)
+        finish(1)
+
+        quantise(xn_mx, 3 * P, P)
         second_multiply(3)
+        finish(2)
         finish(0)
         finish(3, rectifier=nc.vector)

@@ -28,7 +28,7 @@ def tile_l1regressionmoeactionhead_pc_s_kernel(
     nc = tc.nc
     with ExitStack() as ctx:
         keep = ctx.enter_context(tc.tile_pool(name="keep", bufs=1))
-        psum = ctx.enter_context(tc.psum_pool(name="psum", bufs=7))
+        psum = ctx.enter_context(tc.psum_pool(name="psum", bufs=1))
         ctx.enter_context(tc.manual_schedule())
 
         h_view = h_attn.flatten_outer_dims().rearrange("(p j) k -> p j k", j=ROW_TILES)
@@ -61,7 +61,7 @@ def tile_l1regressionmoeactionhead_pc_s_kernel(
         wf_sb = keep.tile([P, ROW_TILES, DIM], BF16)
         load_half(wo_sb, wo_view, 0)
         load_row(nc.sync, b_o_row, 0, b_o)
-        for v, vec in enumerate((gamma, beta, b_ffn)):
+        for v, vec in enumerate((gamma, beta)):
             load_row(nc.scalar, vec_rows, v, vec)
         load_half(x_sb, x_view, 0)
         load_half(wo_sb, wo_view, 1)
@@ -70,6 +70,8 @@ def tile_l1regressionmoeactionhead_pc_s_kernel(
         load_half(h_sb, h_view, 1)
         load_half(wf_sb, wf_view, 0)
         load_half(wf_sb, wf_view, 1)
+        b_ffn_cols = keep.tile([P, PACK], BF16)
+        nc.sync.dma_start(out=b_ffn_cols[:], in_=b_ffn.rearrange("(q t) -> q t", t=PACK))
 
         ident_f32 = keep.tile([P, P], F32)
         make_identity(nc, ident_f32[:])
@@ -82,9 +84,9 @@ def tile_l1regressionmoeactionhead_pc_s_kernel(
             scales = keep.tile([P, ROWS], U8, align_bytes=64, name=name + "_scales")
             return grouped, codes, scales
 
-        def turn(row_tiles, side_by_side=False):
+        def turn(bank_name, row_tiles, side_by_side=False):
             n = len(row_tiles)
-            bank = psum.tile([P, n, 2, P], F32, tag="bank")
+            bank = psum.tile([P, n, 2, P], F32, tag=bank_name)
             for i, rows in enumerate(row_tiles):
                 words = rows.bitcast(F32)
                 for u in range(2):
@@ -125,9 +127,9 @@ def tile_l1regressionmoeactionhead_pc_s_kernel(
                 in_=grouped[:, cols, :].rearrange("p r t -> p (r t)"),
             )
 
-        def multiply(tokens_operand, j, weights_operand):
+        def multiply(bank_name, tokens_operand, j, weights_operand):
             toks = slice(j * P, (j + 1) * P)
-            acc = psum.tile([P, DIM], F32, tag="bank")
+            acc = psum.tile([P, DIM], F32, tag=bank_name)
             nc.tensor.matmul_mx(
                 out=acc[:],
                 lhsT=tokens_operand[1][:, toks].bitcast(FP8X4),
@@ -139,16 +141,16 @@ def tile_l1regressionmoeactionhead_pc_s_kernel(
             )
             return acc
 
-        def columns(rows, n, name):
-            bank = psum.tile([P, 2, P], F32, tag="bank")
+        def columns(bank_name, rows, n, name):
+            bank = psum.tile([P, 2, P], F32, tag=bank_name)
             for u in range(2):
                 nc.tensor.transpose(bank[:, u, :], rows[:].bitcast(F32)[:, u:DIM // 2:2], ident_f32[:])
             cols = keep.tile([P, 2, n], F32, name=name)
             nc.scalar.copy(out=cols[:], in_=bank[:, :, 0:n])
             return cols
 
-        def spread(cols, first, n):
-            bank = psum.tile([P, n, 2, P], F32, tag="bank")
+        def spread(bank_name, cols, first, n):
+            bank = psum.tile([P, n, 2, P], F32, tag=bank_name)
             for i in range(n):
                 for u in range(2):
                     nc.tensor.transpose(
@@ -158,7 +160,7 @@ def tile_l1regressionmoeactionhead_pc_s_kernel(
                     )
             return bank
 
-        busy_bank = psum.tile([P, P], F32, tag="busy", bufs=1)
+        busy_bank = psum.tile([P, P], F32, tag="busy")
 
         def stay_awake(n, rhs):
             for i in range(n):
@@ -185,7 +187,7 @@ def tile_l1regressionmoeactionhead_pc_s_kernel(
         result = keep.tile([P, ROW_TILES, DIM], F32)
 
         stay_awake(2, ones[:])
-        b_o_bank = psum.tile([P, DIM], F32, tag="bank")
+        b_o_bank = psum.tile([P, DIM], F32, tag="a")
         nc.tensor.matmul(b_o_bank[:], lhsT=ones_bf16[:], rhs=b_o_row[:], start=True, stop=True)
         def add_b_o(j):
             nc.vector.tensor_tensor(
@@ -195,20 +197,20 @@ def tile_l1regressionmoeactionhead_pc_s_kernel(
             )
 
         def turn_wo(half):
-            group_wo(half, turn([wo_sb[:, half * HALF_TILES + i, :] for i in range(HALF_TILES)]))
+            group_wo(half, turn("bc"[half], [wo_sb[:, half * HALF_TILES + i, :] for i in range(HALF_TILES)]))
 
         def turn_wf(half):
-            group_wf(half, turn([wf_sb[:, half * HALF_TILES + i, :] for i in range(HALF_TILES)]))
+            group_wf(half, turn("eg"[half], [wf_sb[:, half * HALF_TILES + i, :] for i in range(HALF_TILES)]))
 
         def turn_h(j):
-            group_tile(h_mx, j, turn([h_sb[:, j, :]]))
+            group_tile(h_mx, j, turn("dbgc"[j], [h_sb[:, j, :]]))
 
         accs = {}
         gain_rows = keep.tile([P, 2, DIM], BF16)
         b_ffn_row = keep.tile([P, DIM], BF16)
 
         def first_multiply(j):
-            accs[j] = multiply(h_mx, j, wo_mx)
+            accs[j] = multiply("bacd"[j], h_mx, j, wo_mx)
 
         def copy_gain():
             nc.scalar.copy(
@@ -236,7 +238,7 @@ def tile_l1regressionmoeactionhead_pc_s_kernel(
 
         def negate_mean(first, n):
             cols = slice(first, first + n)
-            nc.vector.tensor_scalar_mul(out=neg_mean[:, cols], in0=y_sum[:, cols], scalar1=-1.0 / DIM)
+            nc.scalar.mul(out=neg_mean[:, cols], in_=y_sum[:, cols], mul=-1.0 / DIM)
 
         def spread_rstd(first, n):
             cols = slice(first, first + n)
@@ -269,12 +271,12 @@ def tile_l1regressionmoeactionhead_pc_s_kernel(
         scaled = keep.tile([P, DIM], F32)
 
         def turn_xn(j):
-            group_tile(xn_mx, j, turn([xn[:, j, :]], side_by_side=True))
+            group_tile(xn_mx, j, turn("daca"[j], [xn[:, j, :]], side_by_side=True))
 
         o_accs = {}
 
         def second_multiply(j):
-            o_accs[j] = multiply(xn_mx, j, wf_mx)
+            o_accs[j] = multiply("fegb"[j], xn_mx, j, wf_mx)
 
         def finish(j, rectifier=nc.scalar):
             if rectifier is nc.scalar:
@@ -292,7 +294,7 @@ def tile_l1regressionmoeactionhead_pc_s_kernel(
 
         turn_wo(0)
         turn_wo(1)
-        vec_cols = columns(vec_rows, 3, "vec_cols")
+        vec_cols = columns("e", vec_rows, 2, "vec_cols")
         stay_awake(1, ones[:])
         add_b_o(0)
         add_b_o(1)
@@ -303,11 +305,8 @@ def tile_l1regressionmoeactionhead_pc_s_kernel(
         quantise(wo_mx, 2 * P, 2 * P)
         turn_h(2)
         turn_h(3)
-        gain_bank = spread(vec_cols, 0, 2)
+        gain_bank = spread("f", vec_cols, 0, 2)
         copy_gain()
-        stay_awake(1, ones[:])
-        b_ffn_bank = spread(vec_cols, 2, 1)
-        copy_b_ffn()
         quantise(h_mx, 0, P)
         add_b_o(3)
         first_multiply(0)
@@ -321,22 +320,25 @@ def tile_l1regressionmoeactionhead_pc_s_kernel(
         first_multiply(3)
         residual(1)
         square(1)
+        negate_mean(0, 2)
         spread_rstd(0, 1)
         residual(2)
         square(2)
-        negate_mean(0, 2)
         normalise_on_gpsimd(0)
         spread_rstd(1, 1)
         residual(3)
+        negate_mean(2, 2)
         square(3)
         gain(1)
-        negate_mean(2, 2)
         normalise(1)
         turn_wf(0)
         spread_rstd(2, 2)
         turn_wf(1)
+        b_ffn_bank = spread("b", b_ffn_cols[:].bitcast(F32).rearrange("p (u v) -> p u v", v=1), 0, 1)
         stay_awake(1, gained[:, 1, 0:P])
         turn_xn(1)
+        copy_b_ffn()
+        stay_awake(1, ones[:])
         gain(2)
         stay_awake(1, gained[:, 2, 0:P])
         gain(3)

@@ -127,9 +127,8 @@ def tile_l1regressionmoeactionhead_pc_s_kernel(
                 in_=grouped[:, cols, :].rearrange("p r t -> p (r t)"),
             )
 
-        def multiply(bank_name, tokens_operand, j, weights_operand):
+        def multiply(acc, tokens_operand, j, weights_operand):
             toks = slice(j * P, (j + 1) * P)
-            acc = psum.tile([P, DIM], F32, tag=bank_name)
             nc.tensor.matmul_mx(
                 out=acc[:],
                 lhsT=tokens_operand[1][:, toks].bitcast(FP8X4),
@@ -140,6 +139,9 @@ def tile_l1regressionmoeactionhead_pc_s_kernel(
                 stop=True,
             )
             return acc
+
+        def product(bank_name):
+            return psum.tile([P, DIM], F32, tag=bank_name, name="product_" + bank_name)
 
         def columns(bank_name, rows, n, name):
             bank = psum.tile([P, 2, P], F32, tag=bank_name)
@@ -160,11 +162,11 @@ def tile_l1regressionmoeactionhead_pc_s_kernel(
                     )
             return bank
 
-        busy_bank = psum.tile([P, P], F32, tag="busy")
+        busy_bank = psum.tile([P, DIM], F32, tag="busy")
 
         def stay_awake(n, rhs):
             for i in range(n):
-                nc.tensor.matmul(busy_bank[:], lhsT=ones[:], rhs=rhs, start=True, stop=True)
+                nc.tensor.matmul(busy_bank[:, 0:P], lhsT=ones[:], rhs=rhs, start=True, stop=True)
 
         def values(bank, v):
             return bank[:, v].rearrange("p u c -> p (u c)").bitcast(BF16)
@@ -209,8 +211,12 @@ def tile_l1regressionmoeactionhead_pc_s_kernel(
         gain_rows = keep.tile([P, 2, DIM], BF16)
         b_ffn_row = keep.tile([P, DIM], BF16)
 
+        def stay_awake_mx(n):
+            for i in range(n):
+                multiply(busy_bank, wo_mx, 0, wo_mx)
+
         def first_multiply(j):
-            accs[j] = multiply("bacd"[j], h_mx, j, wo_mx)
+            accs[j] = multiply(product("bacd"[j]), h_mx, j, wo_mx)
 
         def copy_gain():
             nc.scalar.copy(
@@ -276,7 +282,7 @@ def tile_l1regressionmoeactionhead_pc_s_kernel(
         o_accs = {}
 
         def second_multiply(j):
-            o_accs[j] = multiply("fegb"[j], xn_mx, j, wf_mx)
+            o_accs[j] = multiply(product("fegb"[j]), xn_mx, j, wf_mx)
 
         def finish(j, rectifier=nc.scalar):
             if rectifier is nc.scalar:
@@ -306,6 +312,7 @@ def tile_l1regressionmoeactionhead_pc_s_kernel(
         turn_h(2)
         turn_h(3)
         gain_bank = spread("f", vec_cols, 0, 2)
+        stay_awake(1, ones[:])
         copy_gain()
         quantise(h_mx, 0, P)
         add_b_o(3)
@@ -335,10 +342,11 @@ def tile_l1regressionmoeactionhead_pc_s_kernel(
         spread_rstd(2, 2)
         turn_wf(1)
         b_ffn_bank = spread("b", b_ffn_cols[:].bitcast(F32).rearrange("p (u v) -> p u v", v=1), 0, 1)
+        stay_awake_mx(2)
         stay_awake(1, gained[:, 1, 0:P])
         turn_xn(1)
         copy_b_ffn()
-        stay_awake(1, ones[:])
+        stay_awake_mx(1)
         gain(2)
         stay_awake(1, gained[:, 2, 0:P])
         gain(3)
@@ -349,6 +357,7 @@ def tile_l1regressionmoeactionhead_pc_s_kernel(
         normalise(3)
         turn_xn(0)
         turn_xn(3)
+        stay_awake_mx(1)
         quantise(wf_mx, 0, ROWS)
         quantise(xn_mx, P, P)
         second_multiply(1)

@@ -41,26 +41,27 @@ def tile_l1regressionmoeactionhead_pc_s_kernel(
             tiles = slice(half * HALF_TILES, (half + 1) * HALF_TILES)
             nc.sync.dma_start(out=sb[:, tiles, :], in_=view[:, tiles, :])
 
-        eps = keep.tile([P, 1], F32)
-        nc.vector.memset(eps[:], EPS)
         def load_row(queue, rows, v, vec):
             queue.dma_start(out=rows[v : v + 1, :], in_=vec.rearrange("(u c) -> u c", u=1))
 
+        def load_cols(vec, name):
+            cols = keep.tile([P, PACK], BF16, name=name)
+            nc.sync.dma_start(out=cols[:], in_=vec.rearrange("(q t) -> q t", t=PACK))
+            return cols[:].bitcast(F32).rearrange("p (u v) -> p u v", v=1)
+
         vec_rows = keep.tile([P, DIM], BF16)
         nc.gpsimd.memset(vec_rows[:].bitcast(F32), 0.0)
-        b_o_row = keep.tile([P, DIM], BF16)
-        nc.vector.memset(b_o_row[:].bitcast(F32), 0.0)
         ones = keep.tile([P, P], F32)
         nc.vector.memset(ones[:], 1.0)
-        ones_bf16 = keep.tile([P, P], BF16)
-        nc.vector.memset(ones_bf16[:], 1.0)
+        eps = keep.tile([P, 1], F32)
+        nc.vector.memset(eps[:], EPS)
 
         wo_sb = keep.tile([P, ROW_TILES, DIM], BF16)
         h_sb = keep.tile([P, ROW_TILES, DIM], BF16)
         x_sb = keep.tile([P, ROW_TILES, DIM], BF16)
         wf_sb = keep.tile([P, ROW_TILES, DIM], BF16)
+        b_o_cols = load_cols(b_o, "b_o_cols")
         load_half(wo_sb, wo_view, 0)
-        load_row(nc.sync, b_o_row, 0, b_o)
         for v, vec in enumerate((gamma, beta)):
             load_row(nc.scalar, vec_rows, v, vec)
         load_half(x_sb, x_view, 0)
@@ -70,8 +71,7 @@ def tile_l1regressionmoeactionhead_pc_s_kernel(
         load_half(h_sb, h_view, 1)
         load_half(wf_sb, wf_view, 0)
         load_half(wf_sb, wf_view, 1)
-        b_ffn_cols = keep.tile([P, PACK], BF16)
-        nc.sync.dma_start(out=b_ffn_cols[:], in_=b_ffn.rearrange("(q t) -> q t", t=PACK))
+        b_ffn_cols = load_cols(b_ffn, "b_ffn_cols")
 
         ident_f32 = keep.tile([P, P], F32)
         make_identity(nc, ident_f32[:])
@@ -188,14 +188,14 @@ def tile_l1regressionmoeactionhead_pc_s_kernel(
         biased = keep.tile([P, ROW_TILES, DIM], F32)
         result = keep.tile([P, ROW_TILES, DIM], F32)
 
-        stay_awake(2, ones[:])
-        b_o_bank = psum.tile([P, DIM], F32, tag="a")
-        nc.tensor.matmul(b_o_bank[:], lhsT=ones_bf16[:], rhs=b_o_row[:], start=True, stop=True)
+        stay_awake(3, ones[:])
+        b_o_bank = spread("a", b_o_cols, 0, 1)
+
         def add_b_o(j):
             nc.vector.tensor_tensor(
                 out=xb[:, j, :].rearrange("p (u q e) -> p u q e", u=2, e=2),
                 in0=x_sb[:, j, :].rearrange("p (q u e) -> p u q e", u=2, e=2),
-                in1=b_o_bank[:].rearrange("p (q u e) -> p u q e", u=2, e=2), op=ALU.add,
+                in1=values(b_o_bank, 0).rearrange("p (u q e) -> p u q e", u=2, e=2), op=ALU.add,
             )
 
         def turn_wo(half):
@@ -298,7 +298,9 @@ def tile_l1regressionmoeactionhead_pc_s_kernel(
                     nc.vector.tensor_scalar_max(out=result[:, j, cols], in0=biased[:, j, cols], scalar1=0.0)
             nc.sync.dma_start(out=out_view[:, j, :], in_=result[:, j, :])
 
+        stay_awake(1, ones[:])
         turn_wo(0)
+        stay_awake(1, ones[:])
         turn_wo(1)
         vec_cols = columns("e", vec_rows, 2, "vec_cols")
         stay_awake(1, ones[:])
@@ -307,6 +309,7 @@ def tile_l1regressionmoeactionhead_pc_s_kernel(
         add_b_o(2)
         turn_h(0)
         turn_h(1)
+        stay_awake(1, ones[:])
         quantise(wo_mx, 0, 2 * P)
         quantise(wo_mx, 2 * P, 2 * P)
         turn_h(2)
@@ -341,7 +344,7 @@ def tile_l1regressionmoeactionhead_pc_s_kernel(
         turn_wf(0)
         spread_rstd(2, 2)
         turn_wf(1)
-        b_ffn_bank = spread("b", b_ffn_cols[:].bitcast(F32).rearrange("p (u v) -> p u v", v=1), 0, 1)
+        b_ffn_bank = spread("b", b_ffn_cols, 0, 1)
         stay_awake_mx(2)
         stay_awake(1, gained[:, 1, 0:P])
         turn_xn(1)
@@ -353,7 +356,7 @@ def tile_l1regressionmoeactionhead_pc_s_kernel(
         stay_awake(1, gained[:, 3, 0:P])
         normalise(2)
         turn_xn(2)
-        stay_awake(1, ones[:])
+        stay_awake_mx(1)
         normalise(3)
         turn_xn(0)
         turn_xn(3)

@@ -64,10 +64,10 @@ def tile_l1regressionmoeactionhead_pc_s_kernel(
         load_half(wo_sb, wo_view, 0)
         for v, vec in enumerate((gamma, beta)):
             load_row(nc.scalar, vec_rows, v, vec)
-        load_half(x_sb, x_view, 0)
         load_half(wo_sb, wo_view, 1)
-        load_half(x_sb, x_view, 1)
+        load_half(x_sb, x_view, 0)
         load_half(h_sb, h_view, 0)
+        load_half(x_sb, x_view, 1)
         load_half(h_sb, h_view, 1)
         load_half(wf_sb, wf_view, 0)
         load_half(wf_sb, wf_view, 1)
@@ -324,54 +324,53 @@ def tile_l1regressionmoeactionhead_pc_s_kernel(
         first_multiply(1)
         quantise(h_mx, 2 * P, P)
         first_multiply(2)
-        residual(0)
-        square(0)
         quantise(h_mx, 3 * P, P)
         first_multiply(3)
+        stay_awake_mx(1)
+        stay_awake_mx(1)
+        residual(0)
+        square(0)
         residual(1)
-        square(1)
         negate_mean(0, 2)
         spread_rstd(0, 1)
-        residual(2)
-        square(2)
-        normalise_on_gpsimd(0)
+        square(1)
         spread_rstd(1, 1)
+        normalise_on_gpsimd(0)
+        residual(2)
         residual(3)
         negate_mean(2, 2)
+        square(2)
         square(3)
+        spread_rstd(2, 2)
         gain(1)
+        gain(2)
         normalise(1)
         turn_wf(0)
-        spread_rstd(2, 2)
         turn_wf(1)
         b_ffn_bank = spread("b", b_ffn_cols, 0, 1)
-        stay_awake_mx(2)
-        stay_awake(1, gained[:, 1, 0:P])
-        turn_xn(1)
+        gain(3)
         copy_b_ffn()
         stay_awake_mx(1)
-        gain(2)
-        stay_awake(1, gained[:, 2, 0:P])
-        gain(3)
-        stay_awake(1, gained[:, 3, 0:P])
+        stay_awake_mx(1)
+        turn_xn(1)
+        stay_awake_mx(1)
+        stay_awake_mx(1)
         normalise(2)
         turn_xn(2)
-        stay_awake_mx(1)
         normalise(3)
         turn_xn(0)
         turn_xn(3)
         stay_awake_mx(1)
         quantise(wf_mx, 0, ROWS)
-        quantise(xn_mx, P, P)
+        quantise(xn_mx, 1 * P, P)
         second_multiply(1)
         quantise(xn_mx, 2 * P, P)
         second_multiply(2)
-        quantise(xn_mx, 0, P)
+        quantise(xn_mx, 0 * P, P)
         second_multiply(0)
-        finish(1)
-
         quantise(xn_mx, 3 * P, P)
         second_multiply(3)
+        finish(1)
         finish(2)
-        finish(0)
-        finish(3, rectifier=nc.vector)
+        finish(3)
+        finish(0, rectifier=nc.vector)

from contextlib import ExitStack

import concourse.mybir as mybir
from concourse.masks import make_identity

F32 = mybir.dt.float32
BF16 = mybir.dt.bfloat16
U32 = mybir.dt.uint32
U8 = mybir.dt.uint8
FP8X4 = mybir.dt.float8_e4m3fn_x4
ALU = mybir.AluOpType
ACT = mybir.ActivationFunctionType

P = 128
DIM = 512
ROWS = 512
ROW_TILES = ROWS // P
PACK = 4
HALF_TILES = 2
EPS = 1e-5

FLOPS = 2 * 2 * ROWS * DIM * DIM


def tile_l1regressionmoeactionhead_pc_s_kernel(
    tc, h_attn, x, W_o, b_o, W_ffn, b_ffn, gamma, beta, out
):
    nc = tc.nc
    with ExitStack() as ctx:
        keep = ctx.enter_context(tc.tile_pool(name="keep", bufs=1))
        psum = ctx.enter_context(tc.psum_pool(name="psum", bufs=1))
        ctx.enter_context(tc.manual_schedule())

        h_view = h_attn.flatten_outer_dims().rearrange("(p j) k -> p j k", j=ROW_TILES)
        x_view = x.flatten_outer_dims().rearrange("(p j) o -> p j o", j=ROW_TILES)
        out_view = out.flatten_outer_dims().rearrange("(p j) f -> p j f", j=ROW_TILES)
        wo_view = W_o.rearrange("(p j) k -> p j k", j=ROW_TILES)
        wf_view = W_ffn.rearrange("(p j) k -> p j k", j=ROW_TILES)

        def load_half(sb, view, half):
            tiles = slice(half * HALF_TILES, (half + 1) * HALF_TILES)
            nc.sync.dma_start(out=sb[:, tiles, :], in_=view[:, tiles, :])

        def load_row(queue, rows, v, vec):
            queue.dma_start(out=rows[v : v + 1, :], in_=vec.rearrange("(u c) -> u c", u=1))

        def load_cols(vec, name):
            cols = keep.tile([P, PACK], BF16, name=name)
            nc.sync.dma_start(out=cols[:], in_=vec.rearrange("(q t) -> q t", t=PACK))
            return cols[:].bitcast(F32).rearrange("p (u v) -> p u v", v=1)

        vec_rows = keep.tile([P, DIM], BF16)
        nc.gpsimd.memset(vec_rows[:].bitcast(F32), 0.0)
        ones = keep.tile([P, P], F32)
        nc.vector.memset(ones[:], 1.0)
        eps = keep.tile([P, 1], F32)
        nc.vector.memset(eps[:], EPS)

        wo_sb = keep.tile([P, ROW_TILES, DIM], BF16)
        h_sb = keep.tile([P, ROW_TILES, DIM], BF16)
        x_sb = keep.tile([P, ROW_TILES, DIM], BF16)
        wf_sb = keep.tile([P, ROW_TILES, DIM], BF16)
        b_o_cols = load_cols(b_o, "b_o_cols")
        load_half(wo_sb, wo_view, 0)
        for v, vec in enumerate((gamma, beta)):
            load_row(nc.scalar, vec_rows, v, vec)
        load_half(wo_sb, wo_view, 1)
        load_half(x_sb, x_view, 0)
        load_half(h_sb, h_view, 0)
        load_half(x_sb, x_view, 1)
        load_half(h_sb, h_view, 1)
        load_half(wf_sb, wf_view, 0)
        load_half(wf_sb, wf_view, 1)
        b_ffn_cols = load_cols(b_ffn, "b_ffn_cols")

        ident_f32 = keep.tile([P, P], F32)
        make_identity(nc, ident_f32[:])
        warm = keep.tile([P, 1], F32)
        nc.scalar.activation(out=warm[:], in_=eps[:], func=ACT.Abs_reciprocal_sqrt)

        def mx_tiles(name):
            grouped = keep.tile([P, ROWS, PACK], BF16, align_bytes=64, name=name + "_grouped")
            codes = keep.tile([P, ROWS], U32, align_bytes=64, name=name + "_codes")
            scales = keep.tile([P, ROWS], U8, align_bytes=64, name=name + "_scales")
            return grouped, codes, scales

        def turn(bank_name, row_tiles, side_by_side=False):
            n = len(row_tiles)
            bank = psum.tile([P, n, 2, P], F32, tag=bank_name)
            for i, rows in enumerate(row_tiles):
                words = rows.bitcast(F32)
                for u in range(2):
                    picked = words[:, u * P : (u + 1) * P] if side_by_side else words[:, u : 2 * P : 2]
                    nc.tensor.transpose(bank[:, i, u, :], picked, ident_f32[:])
            return bank

        def words_of(operand):
            return operand[0][:].bitcast(F32)

        def group_tile(operand, j, bank):
            nc.scalar.copy(
                out=words_of(operand)[:, j * P : (j + 1) * P, :],
                in_=bank[:, 0].rearrange("p u r -> p r u"),
            )

        def group_wo(half, bank):
            nc.scalar.copy(
                out=words_of(wo_mx)[:, half * 2 * P : (half + 1) * 2 * P, :].rearrange(
                    "p (r i) u -> p r i u", i=HALF_TILES
                ),
                in_=bank[:].rearrange("p i u r -> p r i u"),
            )

        def group_wf(half, bank):
            tiles = slice(half * HALF_TILES, (half + 1) * HALF_TILES)
            nc.scalar.copy(
                out=words_of(wf_mx).rearrange("p (r j) u -> p r j u", j=ROW_TILES)[:, :, tiles, :],
                in_=bank[:].rearrange("p i u r -> p r i u"),
            )

        def quantise(operand, first_col, n_cols):
            grouped, codes, scales = operand
            cols = slice(first_col, first_col + n_cols)
            nc.vector.quantize_mx(
                out=codes[:, cols].bitcast(FP8X4),
                scales=scales[:, cols],
                in_=grouped[:, cols, :].rearrange("p r t -> p (r t)"),
            )

        def multiply(acc, tokens_operand, j, weights_operand):
            toks = slice(j * P, (j + 1) * P)
            nc.tensor.matmul_mx(
                out=acc[:],
                lhsT=tokens_operand[1][:, toks].bitcast(FP8X4),
                lhsT_scale=tokens_operand[2][:, toks],
                rhs=weights_operand[1][:].bitcast(FP8X4),
                rhs_scale=weights_operand[2][:],
                start=True,
                stop=True,
            )
            return acc

        def product(bank_name):
            return psum.tile([P, DIM], F32, tag=bank_name, name="product_" + bank_name)

        def columns(bank_name, rows, n, name):
            bank = psum.tile([P, 2, P], F32, tag=bank_name)
            for u in range(2):
                nc.tensor.transpose(bank[:, u, :], rows[:].bitcast(F32)[:, u:DIM // 2:2], ident_f32[:])
            cols = keep.tile([P, 2, n], F32, name=name)
            nc.scalar.copy(out=cols[:], in_=bank[:, :, 0:n])
            return cols

        def spread(bank_name, cols, first, n):
            bank = psum.tile([P, n, 2, P], F32, tag=bank_name)
            for i in range(n):
                for u in range(2):
                    nc.tensor.transpose(
                        bank[:, i, u, :],
                        cols[:, u, first + i : first + i + 1].to_broadcast([P, P]),
                        ident_f32[:],
                    )
            return bank

        busy_bank = psum.tile([P, DIM], F32, tag="busy")

        def stay_awake(n, rhs):
            for i in range(n):
                nc.tensor.matmul(busy_bank[:, 0:P], lhsT=ones[:], rhs=rhs, start=True, stop=True)

        def values(bank, v):
            return bank[:, v].rearrange("p u c -> p (u c)").bitcast(BF16)

        wo_mx = mx_tiles("wo")
        h_mx = mx_tiles("h")
        wf_mx = mx_tiles("wf")
        xn_mx = mx_tiles("xn")

        xb = keep.tile([P, ROW_TILES, DIM], F32)
        y = keep.tile([P, ROW_TILES, DIM], F32)
        y_sum = keep.tile([P, ROW_TILES], F32)
        squares = keep.tile([P, ROW_TILES, DIM], BF16)
        sq_sum = keep.tile([P, ROW_TILES], F32)
        neg_mean = keep.tile([P, ROW_TILES], F32)
        rstd = keep.tile([P, ROW_TILES], F32)
        gained = keep.tile([P, ROW_TILES, DIM], F32)
        xn = keep.tile([P, ROW_TILES, DIM], BF16)
        biased = keep.tile([P, ROW_TILES, DIM], F32)
        result = keep.tile([P, ROW_TILES, DIM], F32)

        stay_awake(3, ones[:])
        b_o_bank = spread("a", b_o_cols, 0, 1)

        def add_b_o(j):
            nc.vector.tensor_tensor(
                out=xb[:, j, :].rearrange("p (u q e) -> p u q e", u=2, e=2),
                in0=x_sb[:, j, :].rearrange("p (q u e) -> p u q e", u=2, e=2),
                in1=values(b_o_bank, 0).rearrange("p (u q e) -> p u q e", u=2, e=2), op=ALU.add,
            )

        def turn_wo(half):
            group_wo(half, turn("bc"[half], [wo_sb[:, half * HALF_TILES + i, :] for i in range(HALF_TILES)]))

        def turn_wf(half):
            group_wf(half, turn("eg"[half], [wf_sb[:, half * HALF_TILES + i, :] for i in range(HALF_TILES)]))

        def turn_h(j):
            group_tile(h_mx, j, turn("dbgc"[j], [h_sb[:, j, :]]))

        accs = {}
        gain_rows = keep.tile([P, 2, DIM], BF16)
        b_ffn_row = keep.tile([P, DIM], BF16)

        def stay_awake_mx(n):
            for i in range(n):
                multiply(busy_bank, wo_mx, 0, wo_mx)

        def first_multiply(j):
            accs[j] = multiply(product("bacd"[j]), h_mx, j, wo_mx)

        def copy_gain():
            nc.scalar.copy(
                out=gain_rows[:].bitcast(F32).rearrange("p v w -> p (v w)"),
                in_=gain_bank[:].rearrange("p v u q -> p (v u q)"),
            )

        def copy_b_ffn():
            nc.scalar.copy(
                out=b_ffn_row[:].bitcast(F32).rearrange("p (q u) -> p q u", u=2),
                in_=b_ffn_bank[:, 0].rearrange("p u q -> p q u"),
            )

        def residual(j):
            nc.vector.scalar_tensor_tensor(
                out=y[:, j, :], in0=accs[j][:], scalar=0.0, in1=xb[:, j, :],
                op0=ALU.add, op1=ALU.add, accum_out=y_sum[:, j : j + 1],
            )

        def square(j):
            nc.scalar.activation(
                out=squares[:, j, :], in_=y[:, j, :], func=ACT.Square,
                bias=y_sum[:, j : j + 1], scale=-1.0 * DIM, accum_out=sq_sum[:, j : j + 1],
            )

        def negate_mean(first, n):
            cols = slice(first, first + n)
            nc.scalar.mul(out=neg_mean[:, cols], in_=y_sum[:, cols], mul=-1.0 / DIM)

        def spread_rstd(first, n):
            cols = slice(first, first + n)
            nc.scalar.activation(
                out=rstd[:, cols], in_=sq_sum[:, cols], func=ACT.Abs_reciprocal_sqrt,
                bias=eps[:], scale=1.0 / (DIM * DIM * DIM),
            )

        def gain(j):
            nc.vector.scalar_tensor_tensor(
                out=gained[:, j, :], in0=y[:, j, :],
                scalar=neg_mean[:, j : j + 1], in1=values(gain_bank, 0), op0=ALU.add, op1=ALU.mult,
            )

        def normalise(j):
            nc.vector.scalar_tensor_tensor(
                out=xn[:, j, :], in0=gained[:, j, :],
                scalar=rstd[:, j : j + 1], in1=values(gain_bank, 1), op0=ALU.mult, op1=ALU.add,
            )

        def normalise_on_gpsimd(j):
            nc.gpsimd.tensor_scalar(
                out=centred[:], in0=y[:, j, :], scalar1=neg_mean[:, j : j + 1], scalar2=rstd[:, j : j + 1],
                op0=ALU.add, op1=ALU.mult,
            )
            nc.gpsimd.tensor_tensor(out=scaled[:], in0=centred[:], in1=gain_rows[:, 0, :], op=ALU.mult)
            nc.gpsimd.tensor_tensor(out=xn[:, j, :], in0=scaled[:], in1=gain_rows[:, 1, :], op=ALU.add)

        centred = keep.tile([P, DIM], F32)
        scaled = keep.tile([P, DIM], F32)

        def turn_xn(j):
            group_tile(xn_mx, j, turn("daca"[j], [xn[:, j, :]], side_by_side=True))

        o_accs = {}

        def second_multiply(j):
            o_accs[j] = multiply(product("fegb"[j]), xn_mx, j, wf_mx)

        def finish(j, rectifier=nc.scalar):
            if rectifier is nc.scalar:
                nc.vector.tensor_tensor(out=biased[:, j, :], in0=o_accs[j][:], in1=b_ffn_row[:], op=ALU.add)
                nc.scalar.activation(out=result[:, j, :], in_=biased[:, j, :], func=ACT.Relu)
            else:
                halves = [slice(0, DIM // 2), slice(DIM // 2, DIM)]
                for cols in halves:
                    nc.vector.tensor_tensor(
                        out=biased[:, j, cols], in0=o_accs[j][:, cols], in1=b_ffn_row[:, cols], op=ALU.add
                    )
                for cols in halves:
                    nc.vector.tensor_scalar_max(out=result[:, j, cols], in0=biased[:, j, cols], scalar1=0.0)
            nc.sync.dma_start(out=out_view[:, j, :], in_=result[:, j, :])

        stay_awake(1, ones[:])
        turn_wo(0)
        stay_awake(1, ones[:])
        turn_wo(1)
        vec_cols = columns("e", vec_rows, 2, "vec_cols")
        stay_awake(1, ones[:])
        add_b_o(0)
        add_b_o(1)
        add_b_o(2)
        turn_h(0)
        turn_h(1)
        stay_awake(1, ones[:])
        quantise(wo_mx, 0, 2 * P)
        quantise(wo_mx, 2 * P, 2 * P)
        turn_h(2)
        turn_h(3)
        gain_bank = spread("f", vec_cols, 0, 2)
        stay_awake(1, ones[:])
        copy_gain()
        quantise(h_mx, 0, P)
        add_b_o(3)
        first_multiply(0)
        quantise(h_mx, P, P)
        first_multiply(1)
        quantise(h_mx, 2 * P, P)
        first_multiply(2)
        quantise(h_mx, 3 * P, P)
        first_multiply(3)
        stay_awake_mx(1)
        stay_awake_mx(1)
        residual(0)
        square(0)
        residual(1)
        negate_mean(0, 2)
        spread_rstd(0, 1)
        square(1)
        spread_rstd(1, 1)
        normalise_on_gpsimd(0)
        residual(2)
        residual(3)
        negate_mean(2, 2)
        square(2)
        square(3)
        spread_rstd(2, 2)
        gain(1)
        gain(2)
        normalise(1)
        turn_wf(0)
        turn_wf(1)
        b_ffn_bank = spread("b", b_ffn_cols, 0, 1)
        gain(3)
        copy_b_ffn()
        stay_awake_mx(1)
        stay_awake_mx(1)
        turn_xn(1)
        stay_awake_mx(1)
        stay_awake_mx(1)
        normalise(2)
        turn_xn(2)
        normalise(3)
        turn_xn(0)
        turn_xn(3)
        stay_awake_mx(1)
        quantise(wf_mx, 0, ROWS)
        quantise(xn_mx, 1 * P, P)
        second_multiply(1)
        quantise(xn_mx, 2 * P, P)
        second_multiply(2)
        quantise(xn_mx, 0 * P, P)
        second_multiply(0)
        quantise(xn_mx, 3 * P, P)
        second_multiply(3)
        finish(1)
        finish(2)
        finish(3)
        finish(0, rectifier=nc.vector)
